import numpy as np
import ml_dtypes


def mxq(x, axis, fmt="e4m3"):
    dtype, down = {"e4m3": (ml_dtypes.float8_e4m3fn, 7), "e5m2": (ml_dtypes.float8_e5m2, 14)}[fmt]
    v = np.moveaxis(np.asarray(x, np.float32).astype(ml_dtypes.bfloat16).astype(np.float64), axis, -1)
    blocks = v.reshape(v.shape[:-1] + (-1, 32))
    amax = np.abs(blocks).max(-1, keepdims=True)
    byte = np.maximum(np.where(amax > 0, np.frexp(amax)[1] - 1 + 127, 0) - down, 1)
    scale = np.exp2(byte - 127.0)
    codes = (blocks / scale).astype(np.float32).astype(dtype).astype(np.float64)
    return np.moveaxis((codes * scale).reshape(v.shape), -1, axis)


WIDE = False


def mx_kscale(k):
    if not WIDE:
        return np.ones(k)
    levels = np.array([10, -10, 5, -5, 0])
    a = np.random.permutation(np.resize(levels, k // 512 * 4)).reshape(k // 512, 4)
    idx = np.arange(k)
    return np.exp2(a[idx // 512, idx % 128 // 32])


BF16 = ml_dtypes.bfloat16


def bf(x):
    return np.asarray(x, np.float32).astype(BF16)


def f64(x):
    return np.asarray(x).astype(np.float64)


B, L, DIM, H, D = 2, 128, 2048, 16, 128
EPS = 1e-6
THETA = 10000.0


def rope_table(seq_len, head_dim):
    pos = np.arange(seq_len, dtype=np.float64)
    inv = 1.0 / (THETA ** (np.arange(0, head_dim, 2, dtype=np.float64) / head_dim))
    ang = pos[:, None] * inv[None, :]
    cos, sin = np.cos(ang), np.sin(ang)
    rot = np.stack([np.stack([cos, -sin], -1), np.stack([sin, cos], -1)], -2)
    return rot[None, None]


def rms_norm(u, gain):
    rrms = 1.0 / np.sqrt(np.mean(np.square(u), axis=-1, keepdims=True) + EPS)
    return u * rrms * gain


def rope(u, table):
    ur = u.reshape(*u.shape[:-1], -1, 1, 2)
    out = table[..., 0] * ur[..., 0] + table[..., 1] * ur[..., 1]
    return out.reshape(u.shape)


def setup_inputs():
    s = mx_kscale(DIM)
    return {"x": bf(np.random.standard_normal((B, L, DIM)) * s),
            "pe": bf(rope_table(L, D)),
            "qkv_w": bf(np.random.standard_normal((DIM, 3 * H * D)) / np.sqrt(DIM) / s[:, None]),
            "qkv_b": bf(np.random.standard_normal(3 * H * D) * 0.2),
            "q_scale": bf(1.0 + 0.1 * np.random.standard_normal(D)),
            "k_scale": bf(1.0 + 0.1 * np.random.standard_normal(D))}


def reference(x, pe, qkv_w, qkv_b, q_scale, k_scale):
    qkv = (mxq(f64(x), 2, "e4m3") @ mxq(f64(qkv_w), 0, "e4m3")) + f64(qkv_b)
    qkv = qkv.reshape(B, L, 3, H, D).transpose(2, 0, 3, 1, 4)
    q, k, v = qkv[0], qkv[1], qkv[2]
    q = rms_norm(q, f64(q_scale))
    k = rms_norm(k, f64(k_scale))
    table = f64(pe)
    return rope(q, table), rope(k, table), v

@@ -1,0 +1,260 @@
+from contextlib import ExitStack
+
+import concourse.mybir as mybir
+from concourse.masks import make_identity
+
+F32 = mybir.dt.float32
+BF16 = mybir.dt.bfloat16
+U32 = mybir.dt.uint32
+U8 = mybir.dt.uint8
+FP8X4 = mybir.dt.float8_e4m3fn_x4
+ALU = mybir.AluOpType
+ACT = mybir.ActivationFunctionType
+
+P = 128
+B = 2
+DIM = 2048
+HD = 128
+PASSES = 4
+PIECE = 512
+ROUNDW = 1024
+ROUNDS = 6
+EPS = 1e-6
+FLOPS = 2 * 256 * 2048 * 6144
+
+RAW_BUFS = 10
+AHEAD = 2
+SHARE = ("SVSVSVSV", "SVSSVSVS", "SSVSSSVS", "SVSSVSVS", "SVSSVSVS", "SSVSSSVS")
+WHEN_ADD = 1
+WHEN_SQ = ((2, 3), (3, 4))
+WHEN_ROT = ((4, 5), (6, 7))
+
+
+def tile_selfattention_pa_kernel(tc, x, pe, qkv_w, qkv_b, q_scale, k_scale, out_0, out_1, out_2):
+    nc = tc.nc
+    outs = (out_0, out_1, out_2)
+    with ExitStack() as ctx:
+        ctx.enter_context(tc.manual_schedule())
+        const = ctx.enter_context(tc.tile_pool(name="const", bufs=1))
+        rawp = ctx.enter_context(tc.tile_pool(name="rawp", bufs=RAW_BUFS))
+        grpp = ctx.enter_context(tc.tile_pool(name="grpp", bufs=6))
+        codp = ctx.enter_context(tc.tile_pool(name="codp", bufs=10))
+        yp = ctx.enter_context(tc.tile_pool(name="yp", bufs=6))
+        zp = ctx.enter_context(tc.tile_pool(name="zp", bufs=3))
+        outp = ctx.enter_context(tc.tile_pool(name="outp", bufs=8))
+        smal = ctx.enter_context(tc.tile_pool(name="smal", bufs=4))
+        psum = ctx.enter_context(tc.psum_pool(name="psum", bufs=1))
+
+        n_loads = ROUNDS * PASSES
+        n_pieces = n_loads * 2
+        raws = {}
+        biases = {}
+
+        def load(m):
+            r, c = divmod(m, PASSES)
+            src = qkv_w[512 * c:512 * (c + 1), ROUNDW * r:ROUNDW * (r + 1)].rearrange("(p j) w -> p j w", j=4)
+            if m == 0:
+                for q in range(2):
+                    first = const.tile([P, 4, PIECE], BF16, name="first%d" % q)
+                    nc.sync.dma_start(out=first[:], in_=src[:, :, q * PIECE:(q + 1) * PIECE])
+                    raws[(m, q)] = first[:]
+            else:
+                rw = rawp.tile([P, 4, ROUNDW], BF16, name="rw", tag="rw")
+                nc.sync.dma_start(out=rw[:], in_=src)
+                for q in range(2):
+                    raws[(m, q)] = rw[:, :, q * PIECE:(q + 1) * PIECE]
+            if c == PASSES - 1:
+                b_sb = const.tile([P, ROUNDW], BF16, name="b_sb%d" % r)
+                nc.sync.dma_start(out=b_sb[:], in_=qkv_b[ROUNDW * r:ROUNDW * (r + 1)].partition_broadcast(P))
+                biases[r] = b_sb
+
+        ident = const.tile([P, P], F32, name="ident")
+        make_identity(nc, ident[:])
+        eps = const.tile([P, 1], F32, name="eps")
+        nc.vector.memset(eps[:], EPS)
+
+        load(0)
+        load(1)
+        x_sb = const.tile([P, B, DIM], BF16, name="x_sb")
+        for b in range(B):
+            nc.sync.dma_start(out=x_sb[:, b, :], in_=x[b])
+        for m in range(2, PASSES):
+            load(m)
+        pe_sb = const.tile([P, 256], BF16, name="pe_sb")
+        nc.sync.dma_start(out=pe_sb[:], in_=pe.rearrange("a b l i r c -> (a b l) (i r c)"))
+        gains = []
+        for s, g in enumerate((q_scale, k_scale)):
+            g_sb = const.tile([P, HD], BF16, name="g_sb%d" % s)
+            nc.sync.dma_start(out=g_sb[:], in_=g.partition_broadcast(P))
+            gains.append(g_sb)
+        for m in range(PASSES, RAW_BUFS + 1):
+            load(m)
+
+        xw = x_sb[:].bitcast(F32)
+        xg = const.tile([P, 4 * B * P * PASSES], BF16, name="xg", align_bytes=64)
+        xgw = xg[:].bitcast(F32).rearrange("p (c b r u) -> p c b r u", c=PASSES, b=B, r=P, u=2)
+        xq = const.tile([P, PASSES * B * P], U32, name="xq", align_bytes=64)
+        xs = const.tile([P, PASSES * B * P], U8, name="xs", align_bytes=64)
+
+        def x_turn(cp):
+            for b in range(B):
+                xt = psum.tile([P, 2, 2, P], F32, name="xt", tag="acc1%d%d" % (b, cp))
+                for c2 in range(2):
+                    c = 2 * cp + c2
+                    for u in range(2):
+                        nc.tensor.transpose(xt[:, c2, u, :], xw[:, b, 256 * c + u:256 * (c + 1):2], ident[:])
+                dst = xgw[:, 2 * cp:2 * cp + 2, b, :, :]
+                src = xt[:].rearrange("p c u r -> p c r u")
+                if b == 0:
+                    nc.vector.tensor_copy(out=dst, in_=src)
+                else:
+                    nc.scalar.copy(out=dst, in_=src)
+
+        def x_quantise(cp):
+            nc.vector.quantize_mx(
+                out=xq[:, 512 * cp:512 * (cp + 1)].bitcast(FP8X4),
+                scales=xs[:, 512 * cp:512 * (cp + 1)],
+                in_=xg[:, 2048 * cp:2048 * (cp + 1)],
+            )
+
+        tabs = []
+
+        def tables():
+            for s in range(2):
+                tab = const.tile([P, 2, 64, 2], F32, name="tab%d" % s)
+                nc.vector.tensor_tensor(
+                    out=tab[:],
+                    in0=pe_sb[:].rearrange("p (i r c) -> p r i c", r=2, c=2),
+                    in1=gains[s][:].rearrange("p (i c) -> p i c", c=2).unsqueeze(1).to_broadcast([P, 2, 64, 2]),
+                    op=ALU.mult,
+                )
+                tabs.append(tab)
+
+        grps = {}
+        cods = {}
+        accs = {}
+        agenda = {}
+
+        def later(t, job):
+            agenda[t] = agenda.get(t, []) + [job]
+
+        def where(t):
+            m, nb = divmod(t, 2)
+            r, c = divmod(m, PASSES)
+            return m, r, c, nb
+
+        def regroup(t):
+            m, r, c, nb = where(t)
+            grp = grpp.tile([P, PIECE, 4], BF16, name="grp", tag="grp", align_bytes=64)
+            src = raws[(m, nb)].rearrange("p t (c i) -> p c t i", i=4)
+            dst = grp[:].rearrange("p (c i) t -> p c t i", i=4)
+            if SHARE[r][c * 2 + nb] == "V":
+                nc.vector.tensor_copy(out=dst, in_=src)
+            else:
+                nc.scalar.copy(out=dst, in_=src)
+            grps[t] = grp
+            if nb == 1 and m >= 1 and m + RAW_BUFS < n_loads:
+                load(m + RAW_BUFS)
+
+        def quantise(t):
+            cod = codp.tile([P, PIECE], U32, name="cod", tag="cod", align_bytes=64)
+            scl = codp.tile([P, PIECE], U8, name="scl", tag="scl", align_bytes=64)
+            nc.vector.quantize_mx(out=cod[:].bitcast(FP8X4), scales=scl[:], in_=grps[t][:].rearrange("p w t -> p (w t)"))
+            cods[t] = (cod, scl)
+
+        def store(r, b, nb, o_t):
+            h0 = (r % 2) * 8 + nb * 4
+            nc.sync.dma_start(
+                out=outs[r // 2][b, h0:h0 + 4, :, :].rearrange("h l d -> l h d"),
+                in_=o_t[:].rearrange("p (h d) -> p h d", h=4),
+            )
+
+        def add_bias(r, b, nb, box):
+            pool = outp if r >= 4 else yp
+            y = pool.tile([P, PIECE], F32, name="y", tag="o_t" if r >= 4 else "y")
+            nc.vector.tensor_tensor(out=y[:], in0=accs[(r % 2, b, nb)][:], in1=biases[r][:, PIECE * nb:PIECE * (nb + 1)], op=ALU.add)
+            if r >= 4:
+                store(r, b, nb, y)
+            box["y"] = y
+
+        def squares(box):
+            y = box["y"]
+            ss = smal.tile([P, 4], F32, name="ss", tag="ss")
+            for h in range(4):
+                junk = smal.tile([P, HD], BF16, name="junk", tag="junk")
+                nc.scalar.activation(out=junk[:], in_=y[:, HD * h:HD * (h + 1)], func=ACT.Square, accum_out=ss[:, h:h + 1])
+            rms = smal.tile([P, 4], F32, name="rms", tag="rms")
+            nc.scalar.activation(out=rms[:], in_=ss[:], func=ACT.Sqrt, bias=eps[:], scale=1.0 / HD)
+            box["rms"] = rms
+
+        def rotate(r, b, nb, box):
+            y = box["y"]
+            rr = smal.tile([P, 4], F32, name="rr", tag="rr")
+            nc.vector.reciprocal(out=rr[:], in_=box["rms"][:])
+            z = zp.tile([P, 4, 2, HD], F32, name="z", tag="z")
+            for h in range(4):
+                nc.vector.scalar_tensor_tensor(
+                    out=z[:, h, :, :],
+                    in0=y[:, HD * h:HD * (h + 1)].unsqueeze(1).to_broadcast([P, 2, HD]),
+                    scalar=rr[:, h:h + 1],
+                    in1=tabs[r // 2][:].rearrange("p r i c -> p r (i c)"),
+                    op0=ALU.mult,
+                    op1=ALU.mult,
+                )
+            o_t = outp.tile([P, PIECE], F32, name="o_t", tag="o_t")
+            zv = z[:].rearrange("p h r (i c) -> p h i r c", c=2)
+            nc.vector.tensor_tensor(
+                out=o_t[:].rearrange("p (h i r) -> p h i r", h=4, r=2),
+                in0=zv[:, :, :, :, 0],
+                in1=zv[:, :, :, :, 1],
+                op=ALU.add,
+            )
+            store(r, b, nb, o_t)
+
+        def multiply(t, now):
+            m, r, c, nb = where(t)
+            cod, scl = cods[t]
+            for b in range(B):
+                if c == 0:
+                    accs[(r % 2, b, nb)] = psum.tile([P, PIECE], F32, name="acc", tag="acc%d%d%d" % (r % 2, b, nb))
+                lo = (c * B + b) * P
+                nc.tensor.matmul_mx(
+                    out=accs[(r % 2, b, nb)][:],
+                    lhsT=xq[:, lo:lo + P].bitcast(FP8X4),
+                    lhsT_scale=xs[:, lo:lo + P],
+                    rhs=cod[:].bitcast(FP8X4),
+                    rhs_scale=scl[:],
+                    start=(c == 0),
+                    stop=(c == PASSES - 1),
+                )
+            if c == PASSES - 1:
+                for b in range(B):
+                    box = {}
+                    later(now + WHEN_ADD, lambda r=r, b=b, nb=nb, box=box: add_bias(r, b, nb, box))
+                    if r < 4:
+                        later(now + WHEN_SQ[nb][b], lambda box=box: squares(box))
+                        later(now + WHEN_ROT[nb][b], lambda r=r, b=b, nb=nb, box=box: rotate(r, b, nb, box))
+
+        for t in range(AHEAD):
+            regroup(t)
+        for t in range(n_pieces + 12):
+            if t + AHEAD < n_pieces:
+                regroup(t + AHEAD)
+            if t < n_pieces:
+                quantise(t)
+            if t == 1:
+                x_turn(0)
+                x_turn(1)
+            if t == 2:
+                x_quantise(0)
+                x_quantise(1)
+            if t == 7:
+                tables()
+            if 3 <= t:
+                if t == 3:
+                    multiply(0, t)
+                    multiply(1, t)
+                if t - 1 < n_pieces:
+                    multiply(t - 1, t)
+            for job in agenda.get(t, []):
+                job()

@@ -7,6 +7,7 @@ F32 = mybir.dt.float32
 BF16 = mybir.dt.bfloat16
 U32 = mybir.dt.uint32
 U8 = mybir.dt.uint8
+I32 = mybir.dt.int32
 FP8X4 = mybir.dt.float8_e4m3fn_x4
 ALU = mybir.AluOpType
 ACT = mybir.ActivationFunctionType
@@ -25,6 +26,8 @@ FLOPS = 2 * 256 * 2048 * 6144
 RAW_BUFS = 10
 AHEAD = 2
 SHARE = ("SVSVSVSV", "SVSSVSVS", "SSVSSSVS", "SVSSVSVS", "SVSSVSVS", "SSVSSSVS")
+SPREAD_ORDER = (6, 4, 5, 0, 1, 2, 3)
+SPREAD_TAGS = ("acc000", "acc001", "acc010", "acc011", "acc100", "acc101", "acc110")
 WHEN_ADD = 1
 WHEN_SQ = ((2, 3), (3, 4))
 WHEN_ROT = ((4, 5), (6, 7))
@@ -63,17 +66,20 @@ def tile_selfattention_pa_kernel(tc, x, pe, qkv_w, qkv_b, q_scale, k_scale, out_
                 nc.sync.dma_start(out=rw[:], in_=src)
                 for q in range(2):
                     raws[(m, q)] = rw[:, :, q * PIECE:(q + 1) * PIECE]
-            if c == PASSES - 1:
-                b_sb = const.tile([P, ROUNDW], BF16, name="b_sb%d" % r)
-                nc.sync.dma_start(out=b_sb[:], in_=qkv_b[ROUNDW * r:ROUNDW * (r + 1)].partition_broadcast(P))
-                biases[r] = b_sb
 
         ident = const.tile([P, P], F32, name="ident")
         make_identity(nc, ident[:])
+        identb = const.tile([P, P], BF16, name="identb")
+        make_identity(nc, identb[:])
         eps = const.tile([P, 1], F32, name="eps")
         nc.vector.memset(eps[:], EPS)
+        rows = const.tile([P, PIECE], BF16, name="rows")
+        nc.vector.memset(rows[:].bitcast(I32), 0)
 
         load(0)
+        nc.sync.dma_start(out=rows[0:12, :], in_=qkv_b.rearrange("(j n) -> j n", n=PIECE))
+        nc.sync.dma_start(out=rows[12:13, 0:HD], in_=q_scale.rearrange("(o n) -> o n", o=1))
+        nc.sync.dma_start(out=rows[13:14, 0:HD], in_=k_scale.rearrange("(o n) -> o n", o=1))
         load(1)
         x_sb = const.tile([P, B, DIM], BF16, name="x_sb")
         for b in range(B):
@@ -82,13 +88,33 @@ def tile_selfattention_pa_kernel(tc, x, pe, qkv_w, qkv_b, q_scale, k_scale, out_
             load(m)
         pe_sb = const.tile([P, 256], BF16, name="pe_sb")
         nc.sync.dma_start(out=pe_sb[:], in_=pe.rearrange("a b l i r c -> (a b l) (i r c)"))
-        gains = []
-        for s, g in enumerate((q_scale, k_scale)):
-            g_sb = const.tile([P, HD], BF16, name="g_sb%d" % s)
-            nc.sync.dma_start(out=g_sb[:], in_=g.partition_broadcast(P))
-            gains.append(g_sb)
         for m in range(PASSES, RAW_BUFS + 1):
             load(m)
+
+        g_sb = const.tile([P, 2, HD], BF16, name="g_sb")
+        spread_banks = {}
+
+        def spread(i):
+            bank = psum.tile([P, 2, PIECE], BF16, name="bank", tag=SPREAD_TAGS[i])
+            for h in range(2):
+                j = 2 * i + h
+                nc.tensor.matmul(out=bank[:, h, :], lhsT=identb[:, j:j + 1].to_broadcast([P, P]), rhs=rows[:], start=True, stop=True)
+            spread_banks[i] = bank
+
+        def keep(i):
+            bank = spread_banks[i]
+            if i == 6:
+                nc.scalar.copy(out=g_sb[:], in_=bank[:, :, 0:HD])
+            else:
+                b_sb = const.tile([P, ROUNDW], BF16, name="b_sb%d" % i)
+                if i % 2 == 0:
+                    nc.scalar.copy(out=b_sb[:], in_=bank[:].rearrange("p h n -> p (h n)"))
+                else:
+                    nc.vector.tensor_copy(out=b_sb[:], in_=bank[:].rearrange("p h n -> p (h n)"))
+                biases[i] = b_sb
+
+        for i in SPREAD_ORDER:
+            spread(i)
 
         xw = x_sb[:].bitcast(F32)
         xg = const.tile([P, 4 * B * P * PASSES], BF16, name="xg", align_bytes=64)
@@ -125,7 +151,7 @@ def tile_selfattention_pa_kernel(tc, x, pe, qkv_w, qkv_b, q_scale, k_scale, out_
                 nc.vector.tensor_tensor(
                     out=tab[:],
                     in0=pe_sb[:].rearrange("p (i r c) -> p r i c", r=2, c=2),
-                    in1=gains[s][:].rearrange("p (i c) -> p i c", c=2).unsqueeze(1).to_broadcast([P, 2, 64, 2]),
+                    in1=g_sb[:, s, :].rearrange("p (i c) -> p i c", c=2).unsqueeze(1).to_broadcast([P, 2, 64, 2]),
                     op=ALU.mult,
                 )
                 tabs.append(tab)
@@ -242,6 +268,9 @@ def tile_selfattention_pa_kernel(tc, x, pe, qkv_w, qkv_b, q_scale, k_scale, out_
                 regroup(t + AHEAD)
             if t < n_pieces:
                 quantise(t)
+            if t < 4:
+                for i in SPREAD_ORDER[2 * t:2 * t + 2]:
+                    keep(i)
             if t == 1:
                 x_turn(0)
                 x_turn(1)

@@ -37,7 +37,6 @@ def tile_selfattention_pa_kernel(tc, x, pe, qkv_w, qkv_b, q_scale, k_scale, out_
     nc = tc.nc
     outs = (out_0, out_1, out_2)
     with ExitStack() as ctx:
-        ctx.enter_context(tc.manual_schedule())
         const = ctx.enter_context(tc.tile_pool(name="const", bufs=1))
         rawp = ctx.enter_context(tc.tile_pool(name="rawp", bufs=RAW_BUFS))
         grpp = ctx.enter_context(tc.tile_pool(name="grpp", bufs=6))

@@ -25,7 +25,7 @@ FLOPS = 2 * 256 * 2048 * 6144
 
 RAW_BUFS = 10
 AHEAD = 2
-SHARE = ("SVSVSVSV", "SVSSVSVS", "SSVSSSVS", "SVSSVSVS", "SVSSVSVS", "SSVSSSVS")
+SHARE = ("SVSVSVSV", "SVSVSVSV", "SVSSVSVS", "SVSSVSVS", "SSSSVSSS", "SSVSSSVS")
 SPREAD_ORDER = (6, 4, 5, 0, 1, 2, 3)
 SPREAD_TAGS = ("acc000", "acc001", "acc010", "acc011", "acc100", "acc101", "acc110")
 WHEN_ADD = 1
@@ -130,10 +130,7 @@ def tile_selfattention_pa_kernel(tc, x, pe, qkv_w, qkv_b, q_scale, k_scale, out_
                         nc.tensor.transpose(xt[:, c2, u, :], xw[:, b, 256 * c + u:256 * (c + 1):2], ident[:])
                 dst = xgw[:, 2 * cp:2 * cp + 2, b, :, :]
                 src = xt[:].rearrange("p c u r -> p c r u")
-                if b == 0:
-                    nc.vector.tensor_copy(out=dst, in_=src)
-                else:
-                    nc.scalar.copy(out=dst, in_=src)
+                nc.scalar.copy(out=dst, in_=src)
 
         def x_quantise(cp):
             nc.vector.quantize_mx(
@@ -147,7 +144,7 @@ def tile_selfattention_pa_kernel(tc, x, pe, qkv_w, qkv_b, q_scale, k_scale, out_
         def tables():
             for s in range(2):
                 tab = const.tile([P, 2, 64, 2], F32, name="tab%d" % s)
-                nc.vector.tensor_tensor(
+                nc.gpsimd.tensor_tensor(
                     out=tab[:],
                     in0=pe_sb[:].rearrange("p (i r c) -> p r i c", r=2, c=2),
                     in1=g_sb[:, s, :].rearrange("p (i c) -> p i c", c=2).unsqueeze(1).to_broadcast([P, 2, 64, 2]),
@@ -208,14 +205,13 @@ def tile_selfattention_pa_kernel(tc, x, pe, qkv_w, qkv_b, q_scale, k_scale, out_
             for h in range(4):
                 junk = smal.tile([P, HD], BF16, name="junk", tag="junk")
                 nc.scalar.activation(out=junk[:], in_=y[:, HD * h:HD * (h + 1)], func=ACT.Square, accum_out=ss[:, h:h + 1])
-            rms = smal.tile([P, 4], F32, name="rms", tag="rms")
-            nc.scalar.activation(out=rms[:], in_=ss[:], func=ACT.Sqrt, bias=eps[:], scale=1.0 / HD)
-            box["rms"] = rms
+            rr = smal.tile([P, 4], F32, name="rr", tag="rr")
+            nc.scalar.activation(out=rr[:], in_=ss[:], func=ACT.Abs_reciprocal_sqrt, bias=eps[:], scale=1.0 / HD)
+            box["rr"] = rr
 
         def rotate(r, b, nb, box):
             y = box["y"]
-            rr = smal.tile([P, 4], F32, name="rr", tag="rr")
-            nc.vector.reciprocal(out=rr[:], in_=box["rms"][:])
+            rr = box["rr"]
             z = zp.tile([P, 4, 2, HD], F32, name="z", tag="z")
             for h in range(4):
                 nc.vector.scalar_tensor_tensor(

@@ -20,29 +20,87 @@ PASSES = 4
 PIECE = 512
 ROUNDW = 1024
 ROUNDS = 6
+QK_ROUNDS = 4
+TOK = B * P
 EPS = 1e-6
 FLOPS = 2 * 256 * 2048 * 6144
 
 RAW_BUFS = 10
 AHEAD = 2
-SHARE = ("SVSVSVSV", "SVSVSVSV", "SVSSVSVS", "SVSSVSVS", "SSSSVSSS", "SSVSSSVS")
-SPREAD_ORDER = (6, 4, 5, 0, 1, 2, 3)
-SPREAD_TAGS = ("acc000", "acc001", "acc010", "acc011", "acc100", "acc101", "acc110")
-WHEN_ADD = 1
-WHEN_SQ = ((2, 3), (3, 4))
-WHEN_ROT = ((4, 5), (6, 7))
+COD_BUFS = 18
+L_TAB = 1
+L_TURN = 2
+L_NORM = 3
+L_OUT = 3
+T_PERF = 1
+T_TABS = 2
+T_VBIAS = 5
+T_XT = 3
+T_XQ = 4
+SHARE = ("SVSVSVSV", "SVSVSVSV", "SVSVSVSV", "SVSVSVSV", "SVSVSVSV", "SVSVSVSV")
+
+
+MARK = []
+ORDER = (('R', 0), ('R', 1), ('f', 0), ('Q', 0), ('Q', 1), ('R', 2), ('R', 3), ('t', 0), ('Q', 3), ('x', 0), ('Q', 2), ('x', 1), ('v', 0), ('R', 5), ('R', 4), ('Q', 5), ('L', 11), ('R', 7), ('R', 6), ('Q', 4), ('q', 0), ('L', 12), ('q', 1), ('Q', 7), ('Q', 6), ('P', 0), ('P', 1), ('R', 9), ('L', 13), ('R', 8), ('D', 0), ('Q', 9), ('R', 11), ('R', 10), ('L', 14), ('Q', 8), ('D', 1), ('Q', 11), ('R', 13), ('S', 0), ('P', 2), ('T', 0), ('L', 15), ('R', 12), ('Q', 10), ('Q', 13), ('D', 2), ('S', 1), ('P', 3), ('T', 1), ('R', 15), ('L', 16), ('N', 0), ('S', 2), ('P', 4), ('O', 0), ('R', 14), ('Q', 12), ('T', 2), ('D', 3), ('Q', 15), ('D', 4), ('N', 1), ('S', 3), ('P', 5), ('L', 17), ('O', 1), ('T', 3), ('Q', 14), ('N', 2), ('S', 4), ('P', 6), ('R', 17), ('O', 2), ('R', 16), ('T', 4), ('D', 5), ('Q', 17), ('D', 6), ('N', 3), ('S', 5), ('P', 7), ('R', 19), ('L', 18), ('O', 3), ('T', 5), ('N', 4), ('S', 6), ('P', 8), ('O', 4), ('T', 6), ('Q', 16), ('R', 18), ('D', 7), ('Q', 19), ('D', 8), ('N', 5), ('R', 21), ('S', 7), ('P', 9), ('O', 5), ('T', 7), ('N', 6), ('S', 8), ('P', 10), ('O', 6), ('T', 8), ('Q', 18), ('R', 20), ('Q', 21), ('L', 19), ('D', 9), ('D', 10), ('R', 23), ('N', 7), ('S', 9), ('P', 11), ('O', 7), ('T', 9), ('N', 8), ('S', 10), ('P', 12), ('L', 20), ('Q', 20), ('O', 8), ('T', 10), ('R', 22), ('Q', 23), ('D', 11), ('D', 12), ('R', 25), ('N', 9), ('S', 11), ('P', 13), ('O', 9), ('T', 11), ('N', 10), ('Q', 22), ('S', 12), ('P', 14), ('O', 10), ('T', 12), ('Q', 25), ('R', 24), ('D', 13), ('R', 27), ('N', 11), ('D', 14), ('S', 13), ('P', 15), ('O', 11), ('T', 13), ('Q', 24), ('N', 12), ('S', 14), ('P', 16), ('L', 21), ('O', 12), ('R', 29), ('R', 26), ('T', 14), ('D', 15), ('Q', 27), ('D', 16), ('N', 13), ('S', 15), ('P', 17), ('O', 13), ('T', 15), ('Q', 26), ('N', 14), ('S', 16), ('P', 18), ('Q', 29), ('O', 14), ('R', 28), ('L', 22), ('R', 31), ('T', 16), ('D', 17), ('Q', 31), ('N', 15), ('S', 17), ('P', 19), ('D', 18), ('L', 23), ('O', 15), ('T', 17), ('N', 16), ('Q', 28), ('S', 18), ('P', 20), ('O', 16), ('R', 33), ('R', 30), ('T', 18), ('D', 19), ('Q', 33), ('N', 17), ('D', 20), ('S', 19), ('P', 21), ('O', 17), ('T', 19), ('Q', 30), ('N', 18), ('S', 20), ('P', 22), ('O', 18), ('R', 35), ('R', 32), ('T', 20), ('D', 21), ('R', 37), ('N', 19), ('S', 21), ('P', 23), ('D', 22), ('O', 19), ('T', 21), ('N', 20), ('S', 22), ('P', 24), ('Q', 32), ('O', 20), ('R', 34), ('Q', 37), ('T', 22), ('D', 23), ('Q', 35), ('D', 24), ('M', 32), ('N', 21), ('S', 23), ('P', 25), ('R', 39), ('O', 21), ('T', 23), ('N', 22), ('S', 24), ('P', 26), ('O', 22), ('T', 24), ('Q', 34), ('R', 36), ('D', 25), ('Q', 39), ('M', 33), ('D', 26), ('N', 23), ('R', 41), ('S', 25), ('P', 27), ('O', 23), ('T', 25), ('N', 24), ('S', 26), ('O', 24), ('Q', 36), ('R', 38), ('Q', 41), ('M', 34), ('D', 27), ('T', 26), ('R', 43), ('P', 28), ('N', 25), ('S', 27), ('Q', 38), ('O', 25), ('M', 35), ('N', 26), ('R', 40), ('D', 28), ('T', 27), ('R', 45), ('P', 29), ('R', 47), ('S', 28), ('M', 36), ('O', 26), ('N', 27), ('S', 29), ('D', 29), ('T', 28), ('O', 27), ('Q', 40), ('R', 42), ('P', 30), ('M', 37), ('D', 30), ('N', 28), ('T', 29), ('S', 30), ('Q', 42), ('O', 28), ('R', 44), ('P', 31), ('Q', 43), ('M', 38), ('D', 31), ('T', 30), ('A', 0), ('N', 29), ('S', 31), ('O', 29), ('A', 1), ('R', 46), ('M', 39), ('Q', 44), ('T', 31), ('A', 2), ('A', 3), ('Q', 45), ('M', 40), ('N', 30), ('N', 31), ('O', 30), ('Q', 46), ('M', 41), ('O', 31), ('Q', 47), ('M', 42), ('M', 43), ('M', 44), ('M', 45), ('M', 46), ('A', 4), ('M', 47), ('A', 5), ('A', 6), ('A', 7))
+
+
+def default_order():
+    order = []
+    n_pieces = 48
+    n_heads = 32
+
+    def head(name, g):
+        if 0 <= g < n_heads:
+            order.append((name, g))
+
+    def piece(t):
+        order.append(("R", t))
+        m, nb = divmod(t, 2)
+        if nb == 1 and m >= 1 and m + RAW_BUFS < 24:
+            order.append(("L", m + RAW_BUFS))
+
+    for t in range(AHEAD):
+        piece(t)
+    for t in range(n_pieces + 12):
+        g = t - 8
+        head("N", g - L_NORM)
+        head("T", g - L_TURN)
+        head("P", g)
+        if t < n_pieces:
+            order.append(("Q", t))
+        head("D", g - L_TAB)
+        if t + AHEAD < n_pieces:
+            piece(t + AHEAD)
+        head("S", g - L_TAB)
+        head("O", g - L_OUT)
+        if t == T_PERF:
+            order.append(("f", 0))
+        if t == T_TABS:
+            order.append(("t", 0))
+        if t == T_VBIAS:
+            order.append(("v", 0))
+        if t == T_XT:
+            order.extend([("x", 0), ("x", 1)])
+        if t == T_XQ:
+            order.extend([("q", 0), ("q", 1)])
+        if 33 <= t <= n_pieces:
+            order.append(("M", t - 1))
+            if (t - 1) % 8 >= 6:
+                k = ((t - 1) // 8 - 4) * 4 + ((t - 1) % 2) * 2
+                order.extend([("A", k), ("A", k + 1)])
+    return order
 
 
 def tile_selfattention_pa_kernel(tc, x, pe, qkv_w, qkv_b, q_scale, k_scale, out_0, out_1, out_2):
     nc = tc.nc
     outs = (out_0, out_1, out_2)
     with ExitStack() as ctx:
+        ctx.enter_context(tc.manual_schedule())
         const = ctx.enter_context(tc.tile_pool(name="const", bufs=1))
         rawp = ctx.enter_context(tc.tile_pool(name="rawp", bufs=RAW_BUFS))
         grpp = ctx.enter_context(tc.tile_pool(name="grpp", bufs=6))
-        codp = ctx.enter_context(tc.tile_pool(name="codp", bufs=10))
-        yp = ctx.enter_context(tc.tile_pool(name="yp", bufs=6))
-        zp = ctx.enter_context(tc.tile_pool(name="zp", bufs=3))
+        codp = ctx.enter_context(tc.tile_pool(name="codp", bufs=COD_BUFS))
+        dop = ctx.enter_context(tc.tile_pool(name="dop", bufs=4))
         outp = ctx.enter_context(tc.tile_pool(name="outp", bufs=8))
         smal = ctx.enter_context(tc.tile_pool(name="smal", bufs=4))
         psum = ctx.enter_context(tc.psum_pool(name="psum", bufs=1))
@@ -70,50 +128,66 @@ def tile_selfattention_pa_kernel(tc, x, pe, qkv_w, qkv_b, q_scale, k_scale, out_
         make_identity(nc, ident[:])
         identb = const.tile([P, P], BF16, name="identb")
         make_identity(nc, identb[:])
+        swp = const.tile([P, 64, 2], F32, name="swp")
+        idv = ident[:].rearrange("p (i c) -> p i c", c=2)
+        nc.gpsimd.tensor_copy(out=swp[:, :, 0], in_=idv[:, :, 1])
+        nc.gpsimd.tensor_copy(out=swp[:, :, 1], in_=idv[:, :, 0])
         eps = const.tile([P, 1], F32, name="eps")
         nc.vector.memset(eps[:], EPS)
-        rows = const.tile([P, PIECE], BF16, name="rows")
-        nc.vector.memset(rows[:].bitcast(I32), 0)
+        ones = const.tile([P, P], F32, name="ones")
+        nc.vector.memset(ones[:], 1.0)
+        hrows = const.tile([P, P], BF16, name="hrows")
+        nc.vector.memset(hrows[:].bitcast(I32), 0)
+        vrows = const.tile([P, PIECE], BF16, name="vrows")
+        nc.vector.memset(vrows[:].bitcast(I32), 0)
 
         load(0)
-        nc.sync.dma_start(out=rows[0:12, :], in_=qkv_b.rearrange("(j n) -> j n", n=PIECE))
-        nc.sync.dma_start(out=rows[12:13, 0:HD], in_=q_scale.rearrange("(o n) -> o n", o=1))
-        nc.sync.dma_start(out=rows[13:14, 0:HD], in_=k_scale.rearrange("(o n) -> o n", o=1))
+        nc.sync.dma_start(out=hrows[0:32, :], in_=qkv_b[0:4096].rearrange("(j n) -> j n", n=HD))
+        nc.sync.dma_start(out=hrows[32:33, :], in_=q_scale.rearrange("(o n) -> o n", o=1))
+        nc.sync.dma_start(out=hrows[33:34, :], in_=k_scale.rearrange("(o n) -> o n", o=1))
+        pe_sb = const.tile([P, 256], BF16, name="pe_sb")
+        nc.sync.dma_start(out=pe_sb[:], in_=pe.rearrange("a b l i r c -> (a b l) (i r c)"))
         load(1)
         x_sb = const.tile([P, B, DIM], BF16, name="x_sb")
         for b in range(B):
             nc.sync.dma_start(out=x_sb[:, b, :], in_=x[b])
-        for m in range(2, PASSES):
-            load(m)
-        pe_sb = const.tile([P, 256], BF16, name="pe_sb")
-        nc.sync.dma_start(out=pe_sb[:], in_=pe.rearrange("a b l i r c -> (a b l) (i r c)"))
-        for m in range(PASSES, RAW_BUFS + 1):
+        nc.sync.dma_start(out=vrows[0:4, :], in_=qkv_b[4096:6144].rearrange("(j n) -> j n", n=PIECE))
+        for m in range(2, RAW_BUFS + 1):
             load(m)
 
-        g_sb = const.tile([P, 2, HD], BF16, name="g_sb")
-        spread_banks = {}
+        per_f = const.tile([P, 34], F32, name="per_f")
+        pel = const.tile([P, 2, 64, 2], F32, name="pel")
+        tabs = []
+        setup = {}
 
-        def spread(i):
-            bank = psum.tile([P, 2, PIECE], BF16, name="bank", tag=SPREAD_TAGS[i])
-            for h in range(2):
-                j = 2 * i + h
-                nc.tensor.matmul(out=bank[:, h, :], lhsT=identb[:, j:j + 1].to_broadcast([P, P]), rhs=rows[:], start=True, stop=True)
-            spread_banks[i] = bank
+        def per_feature():
+            hps = psum.tile([P, P], BF16, name="hps", tag="rb", bufs=2)
+            nc.tensor.transpose(hps[:], hrows[:], identb[:])
+            nc.vector.tensor_copy(out=per_f[:], in_=hps[:, 0:34])
+            pev = pe_sb[:].rearrange("p (i x) -> p i x", x=4)
+            nc.vector.tensor_copy(out=pel[:, 0, :, :], in_=pev[:, :, 0:4:3])
+            nc.vector.tensor_copy(out=pel[:, 1, :, 0], in_=pev[:, :, 2])
+            nc.vector.tensor_copy(out=pel[:, 1, :, 1], in_=pev[:, :, 1])
 
-        def keep(i):
-            bank = spread_banks[i]
-            if i == 6:
-                nc.scalar.copy(out=g_sb[:], in_=bank[:, :, 0:HD])
-            else:
+        def tables():
+            tps = psum.tile([P, 2, P], F32, name="tps", tag="rb", bufs=2)
+            for d in range(2):
+                nc.tensor.transpose(tps[:, d, :], pel[:, d, :, :].rearrange("p i c -> p (i c)"), ident[:])
+            for s in range(2):
+                tab = const.tile([P, 2, B, P], F32, name="tab%d" % s)
+                for b in range(B):
+                    nc.scalar.activation(out=tab[:, :, b, :], in_=tps[:], func=ACT.Copy, scale=per_f[:, 32 + s:33 + s])
+                tabs.append(tab)
+
+        def v_bias():
+            for i in range(2):
+                bank = psum.tile([P, 2, PIECE], BF16, name="bank", tag="pt", bufs=2)
+                for h in range(2):
+                    j = 2 * i + h
+                    nc.tensor.matmul(out=bank[:, h, :], lhsT=identb[:, j:j + 1].to_broadcast([P, P]), rhs=vrows[:], start=True, stop=True)
                 b_sb = const.tile([P, ROUNDW], BF16, name="b_sb%d" % i)
-                if i % 2 == 0:
-                    nc.scalar.copy(out=b_sb[:], in_=bank[:].rearrange("p h n -> p (h n)"))
-                else:
-                    nc.vector.tensor_copy(out=b_sb[:], in_=bank[:].rearrange("p h n -> p (h n)"))
-                biases[i] = b_sb
-
-        for i in SPREAD_ORDER:
-            spread(i)
+                nc.scalar.copy(out=b_sb[:], in_=bank[:].rearrange("p h n -> p (h n)"))
+                biases[QK_ROUNDS + i] = b_sb
 
         xw = x_sb[:].bitcast(F32)
         xg = const.tile([P, 4 * B * P * PASSES], BF16, name="xg", align_bytes=64)
@@ -123,14 +197,12 @@ def tile_selfattention_pa_kernel(tc, x, pe, qkv_w, qkv_b, q_scale, k_scale, out_
 
         def x_turn(cp):
             for b in range(B):
-                xt = psum.tile([P, 2, 2, P], F32, name="xt", tag="acc1%d%d" % (b, cp))
+                xt = psum.tile([P, 2, 2, P], F32, name="xt", tag="va%d%d" % (b, cp))
                 for c2 in range(2):
                     c = 2 * cp + c2
                     for u in range(2):
                         nc.tensor.transpose(xt[:, c2, u, :], xw[:, b, 256 * c + u:256 * (c + 1):2], ident[:])
-                dst = xgw[:, 2 * cp:2 * cp + 2, b, :, :]
-                src = xt[:].rearrange("p c u r -> p c r u")
-                nc.scalar.copy(out=dst, in_=src)
+                nc.scalar.copy(out=xgw[:, 2 * cp:2 * cp + 2, b, :, :], in_=xt[:].rearrange("p c u r -> p c r u"))
 
         def x_quantise(cp):
             nc.vector.quantize_mx(
@@ -138,19 +210,6 @@ def tile_selfattention_pa_kernel(tc, x, pe, qkv_w, qkv_b, q_scale, k_scale, out_
                 scales=xs[:, 512 * cp:512 * (cp + 1)],
                 in_=xg[:, 2048 * cp:2048 * (cp + 1)],
             )
-
-        tabs = []
-
-        def tables():
-            for s in range(2):
-                tab = const.tile([P, 2, 64, 2], F32, name="tab%d" % s)
-                nc.gpsimd.tensor_tensor(
-                    out=tab[:],
-                    in0=pe_sb[:].rearrange("p (i r c) -> p r i c", r=2, c=2),
-                    in1=g_sb[:, s, :].rearrange("p (i c) -> p i c", c=2).unsqueeze(1).to_broadcast([P, 2, 64, 2]),
-                    op=ALU.mult,
-                )
-                tabs.append(tab)
 
         grps = {}
         cods = {}
@@ -175,14 +234,13 @@ def tile_selfattention_pa_kernel(tc, x, pe, qkv_w, qkv_b, q_scale, k_scale, out_
             else:
                 nc.scalar.copy(out=dst, in_=src)
             grps[t] = grp
-            if nb == 1 and m >= 1 and m + RAW_BUFS < n_loads:
-                load(m + RAW_BUFS)
 
         def quantise(t):
+            m, r, c, nb = where(t)
             cod = codp.tile([P, PIECE], U32, name="cod", tag="cod", align_bytes=64)
             scl = codp.tile([P, PIECE], U8, name="scl", tag="scl", align_bytes=64)
             nc.vector.quantize_mx(out=cod[:].bitcast(FP8X4), scales=scl[:], in_=grps[t][:].rearrange("p w t -> p (w t)"))
-            cods[t] = (cod, scl)
+            cods[(r, c, nb)] = (cod, scl)
 
         def store(r, b, nb, o_t):
             h0 = (r % 2) * 8 + nb * 4
@@ -191,56 +249,87 @@ def tile_selfattention_pa_kernel(tc, x, pe, qkv_w, qkv_b, q_scale, k_scale, out_
                 in_=o_t[:].rearrange("p (h d) -> p h d", h=4),
             )
 
-        def add_bias(r, b, nb, box):
-            pool = outp if r >= 4 else yp
-            y = pool.tile([P, PIECE], F32, name="y", tag="o_t" if r >= 4 else "y")
-            nc.vector.tensor_tensor(out=y[:], in0=accs[(r % 2, b, nb)][:], in1=biases[r][:, PIECE * nb:PIECE * (nb + 1)], op=ALU.add)
-            if r >= 4:
-                store(r, b, nb, y)
-            box["y"] = y
+        live = {}
 
-        def squares(box):
-            y = box["y"]
-            ss = smal.tile([P, 4], F32, name="ss", tag="ss")
-            for h in range(4):
-                junk = smal.tile([P, HD], BF16, name="junk", tag="junk")
-                nc.scalar.activation(out=junk[:], in_=y[:, HD * h:HD * (h + 1)], func=ACT.Square, accum_out=ss[:, h:h + 1])
-            rr = smal.tile([P, 4], F32, name="rr", tag="rr")
-            nc.scalar.activation(out=rr[:], in_=ss[:], func=ACT.Abs_reciprocal_sqrt, bias=eps[:], scale=1.0 / HD)
-            box["rr"] = rr
-
-        def rotate(r, b, nb, box):
-            y = box["y"]
-            rr = box["rr"]
-            z = zp.tile([P, 4, 2, HD], F32, name="z", tag="z")
-            for h in range(4):
-                nc.vector.scalar_tensor_tensor(
-                    out=z[:, h, :, :],
-                    in0=y[:, HD * h:HD * (h + 1)].unsqueeze(1).to_broadcast([P, 2, HD]),
-                    scalar=rr[:, h:h + 1],
-                    in1=tabs[r // 2][:].rearrange("p r i c -> p r (i c)"),
-                    op0=ALU.mult,
-                    op1=ALU.mult,
+        def head_project(g):
+            r, j = divmod(g, 8)
+            nb, hh = divmod(j, 4)
+            pt = psum.tile([P, TOK], F32, name="pt", tag="pt", bufs=2)
+            live[("pt", g)] = pt
+            for c in range(PASSES):
+                cod, scl = cods[(r, c, nb)]
+                nc.tensor.matmul_mx(
+                    out=pt[:],
+                    lhsT=cod[:, hh * HD:(hh + 1) * HD].bitcast(FP8X4),
+                    lhsT_scale=scl[:, hh * HD:(hh + 1) * HD],
+                    rhs=xq[:, TOK * c:TOK * (c + 1)].bitcast(FP8X4),
+                    rhs_scale=xs[:, TOK * c:TOK * (c + 1)],
+                    start=(c == 0),
+                    stop=(c == PASSES - 1),
                 )
-            o_t = outp.tile([P, PIECE], F32, name="o_t", tag="o_t")
-            zv = z[:].rearrange("p h r (i c) -> p h i r c", c=2)
-            nc.vector.tensor_tensor(
-                out=o_t[:].rearrange("p (h i r) -> p h i r", h=4, r=2),
-                in0=zv[:, :, :, :, 0],
-                in1=zv[:, :, :, :, 1],
-                op=ALU.add,
+
+        def head_tables(g):
+            pt = live[("pt", g)]
+            do = dop.tile([P, 2, TOK], F32, name="do", tag="do")
+            nc.vector.scalar_tensor_tensor(
+                out=do[:],
+                in0=pt[:].unsqueeze(1).to_broadcast([P, 2, TOK]),
+                scalar=per_f[:, g:g + 1],
+                in1=tabs[g // 16][:].rearrange("p d b l -> p d (b l)"),
+                op0=ALU.add,
+                op1=ALU.mult,
             )
+            live[("do", g)] = do
+
+        def head_squares(g):
+            pt = live[("pt", g)]
+            sq = dop.tile([P, TOK], F32, name="sq", tag="sq")
+            nc.scalar.activation(out=sq[:], in_=pt[:], func=ACT.Square, bias=per_f[:, g:g + 1], scale=1.0)
+            live[("sq", g)] = sq
+
+        def head_turn(g):
+            rb = psum.tile([P, 4, P], F32, name="rb", tag="rb", bufs=2)
+            for b in range(B):
+                nc.tensor.matmul(out=rb[:, 2 + b, :], lhsT=live[("sq", g)][:, P * b:P * (b + 1)], rhs=ones[:], start=True, stop=True)
+            for b in range(B):
+                tok = slice(P * b, P * (b + 1))
+                nc.tensor.matmul(out=rb[:, b, :], lhsT=live[("do", g)][:, 0, tok], rhs=ident[:], is_transpose=True, start=True, stop=False)
+                nc.tensor.matmul(out=rb[:, b, :], lhsT=live[("do", g)][:, 1, tok], rhs=swp[:].rearrange("p i c -> p (i c)"), is_transpose=True, start=False, stop=True)
+            live[("rb", g)] = rb
+
+        def head_norm(g):
+            rr = smal.tile([P, 2], F32, name="rr", tag="rr")
+            nc.scalar.activation(out=rr[:], in_=live[("rb", g)][:, 2:4, 0], func=ACT.Abs_reciprocal_sqrt, bias=eps[:], scale=1.0 / HD)
+            live[("rr", g)] = rr
+
+        def head_out(g):
+            r, j = divmod(g, 8)
+            nb, hh = divmod(j, 4)
+            for b in range(B):
+                if hh == 0:
+                    live[("o", g // 4, b)] = outp.tile([P, PIECE], F32, name="o_t", tag="o_t")
+                o_t = live[("o", g // 4, b)]
+                nc.scalar.activation(out=o_t[:, hh * HD:(hh + 1) * HD], in_=live[("rb", g)][:, b, :], func=ACT.Copy, scale=live[("rr", g)][:, b:b + 1])
+                if hh == 3:
+                    store(r, b, nb, o_t)
+
+        def add_bias(k):
+            r, rest = divmod(k, 4)
+            nb, b = divmod(rest, 2)
+            r += QK_ROUNDS
+            o_t = outp.tile([P, PIECE], F32, name="o_t", tag="o_t")
+            nc.vector.tensor_tensor(out=o_t[:], in0=accs[(b, nb)][:], in1=biases[r][:, PIECE * nb:PIECE * (nb + 1)], op=ALU.add)
             store(r, b, nb, o_t)
 
-        def multiply(t, now):
+        def multiply(t):
             m, r, c, nb = where(t)
-            cod, scl = cods[t]
+            cod, scl = cods[(r, c, nb)]
             for b in range(B):
                 if c == 0:
-                    accs[(r % 2, b, nb)] = psum.tile([P, PIECE], F32, name="acc", tag="acc%d%d%d" % (r % 2, b, nb))
+                    accs[(b, nb)] = psum.tile([P, PIECE], F32, name="acc", tag="va%d%d" % (b, nb))
                 lo = (c * B + b) * P
                 nc.tensor.matmul_mx(
-                    out=accs[(r % 2, b, nb)][:],
+                    out=accs[(b, nb)][:],
                     lhsT=xq[:, lo:lo + P].bitcast(FP8X4),
                     lhsT_scale=xs[:, lo:lo + P],
                     rhs=cod[:].bitcast(FP8X4),
@@ -248,37 +337,12 @@ def tile_selfattention_pa_kernel(tc, x, pe, qkv_w, qkv_b, q_scale, k_scale, out_
                     start=(c == 0),
                     stop=(c == PASSES - 1),
                 )
-            if c == PASSES - 1:
-                for b in range(B):
-                    box = {}
-                    later(now + WHEN_ADD, lambda r=r, b=b, nb=nb, box=box: add_bias(r, b, nb, box))
-                    if r < 4:
-                        later(now + WHEN_SQ[nb][b], lambda box=box: squares(box))
-                        later(now + WHEN_ROT[nb][b], lambda r=r, b=b, nb=nb, box=box: rotate(r, b, nb, box))
 
-        for t in range(AHEAD):
-            regroup(t)
-        for t in range(n_pieces + 12):
-            if t + AHEAD < n_pieces:
-                regroup(t + AHEAD)
-            if t < n_pieces:
-                quantise(t)
-            if t < 4:
-                for i in SPREAD_ORDER[2 * t:2 * t + 2]:
-                    keep(i)
-            if t == 1:
-                x_turn(0)
-                x_turn(1)
-            if t == 2:
-                x_quantise(0)
-                x_quantise(1)
-            if t == 7:
-                tables()
-            if 3 <= t:
-                if t == 3:
-                    multiply(0, t)
-                    multiply(1, t)
-                if t - 1 < n_pieces:
-                    multiply(t - 1, t)
-            for job in agenda.get(t, []):
-                job()
+        steps = {
+            "L": load, "R": regroup, "Q": quantise, "P": head_project, "D": head_tables, "S": head_squares,
+            "T": head_turn, "N": head_norm, "O": head_out, "M": multiply, "A": add_bias,
+            "f": lambda k: per_feature(), "t": lambda k: tables(), "v": lambda k: v_bias(), "x": x_turn, "q": x_quantise,
+        }
+        for name, k in ORDER or default_order():
+            MARK.append((name, k))
+            steps[name](k)

@@ -17,112 +17,123 @@ B = 2
 DIM = 2048
 HD = 128
 PASSES = 4
-PIECE = 512
-ROUNDW = 1024
-ROUNDS = 6
-QK_ROUNDS = 4
+BLK = 512
 TOK = B * P
 EPS = 1e-6
 FLOPS = 2 * 256 * 2048 * 6144
 
-RAW_BUFS = 10
-AHEAD = 2
-COD_BUFS = 18
-L_TAB = 1
-L_TURN = 2
-L_NORM = 3
-L_OUT = 3
-T_PERF = 1
-T_TABS = 2
-T_VBIAS = 5
-T_XT = 3
-T_XQ = 4
-SHARE = ("SVSVSVSV", "SVSVSVSV", "SVSVSVSV", "SVSVSVSV", "SVSVSVSV", "SVSVSVSV")
+N_QK = 8
+N_V = 4
+SS_N = 64
+HALF_BUFS = 8
+FULL_BUFS = 6
+GRP_BUFS = 4
+COD_BUFS = 8
+AHEAD_S = 2
+AHEAD_V = 1
+LAG_D = 1
+LAG_SQ = 1
+LAG_O = 3
+POOL_COLS = 0
+PT_BUFS = 3
 
 
-MARK = []
-ORDER = (('R', 0), ('R', 1), ('f', 0), ('Q', 0), ('Q', 1), ('R', 2), ('R', 3), ('t', 0), ('Q', 3), ('x', 0), ('Q', 2), ('x', 1), ('v', 0), ('R', 5), ('R', 4), ('Q', 5), ('L', 11), ('R', 7), ('R', 6), ('Q', 4), ('q', 0), ('L', 12), ('q', 1), ('Q', 7), ('Q', 6), ('P', 0), ('P', 1), ('R', 9), ('L', 13), ('R', 8), ('D', 0), ('Q', 9), ('R', 11), ('R', 10), ('L', 14), ('Q', 8), ('D', 1), ('Q', 11), ('R', 13), ('S', 0), ('P', 2), ('T', 0), ('L', 15), ('R', 12), ('Q', 10), ('Q', 13), ('D', 2), ('S', 1), ('P', 3), ('T', 1), ('R', 15), ('L', 16), ('N', 0), ('S', 2), ('P', 4), ('O', 0), ('R', 14), ('Q', 12), ('T', 2), ('D', 3), ('Q', 15), ('D', 4), ('N', 1), ('S', 3), ('P', 5), ('L', 17), ('O', 1), ('T', 3), ('Q', 14), ('N', 2), ('S', 4), ('P', 6), ('R', 17), ('O', 2), ('R', 16), ('T', 4), ('D', 5), ('Q', 17), ('D', 6), ('N', 3), ('S', 5), ('P', 7), ('R', 19), ('L', 18), ('O', 3), ('T', 5), ('N', 4), ('S', 6), ('P', 8), ('O', 4), ('T', 6), ('Q', 16), ('R', 18), ('D', 7), ('Q', 19), ('D', 8), ('N', 5), ('R', 21), ('S', 7), ('P', 9), ('O', 5), ('T', 7), ('N', 6), ('S', 8), ('P', 10), ('O', 6), ('T', 8), ('Q', 18), ('R', 20), ('Q', 21), ('L', 19), ('D', 9), ('D', 10), ('R', 23), ('N', 7), ('S', 9), ('P', 11), ('O', 7), ('T', 9), ('N', 8), ('S', 10), ('P', 12), ('L', 20), ('Q', 20), ('O', 8), ('T', 10), ('R', 22), ('Q', 23), ('D', 11), ('D', 12), ('R', 25), ('N', 9), ('S', 11), ('P', 13), ('O', 9), ('T', 11), ('N', 10), ('Q', 22), ('S', 12), ('P', 14), ('O', 10), ('T', 12), ('Q', 25), ('R', 24), ('D', 13), ('R', 27), ('N', 11), ('D', 14), ('S', 13), ('P', 15), ('O', 11), ('T', 13), ('Q', 24), ('N', 12), ('S', 14), ('P', 16), ('L', 21), ('O', 12), ('R', 29), ('R', 26), ('T', 14), ('D', 15), ('Q', 27), ('D', 16), ('N', 13), ('S', 15), ('P', 17), ('O', 13), ('T', 15), ('Q', 26), ('N', 14), ('S', 16), ('P', 18), ('Q', 29), ('O', 14), ('R', 28), ('L', 22), ('R', 31), ('T', 16), ('D', 17), ('Q', 31), ('N', 15), ('S', 17), ('P', 19), ('D', 18), ('L', 23), ('O', 15), ('T', 17), ('N', 16), ('Q', 28), ('S', 18), ('P', 20), ('O', 16), ('R', 33), ('R', 30), ('T', 18), ('D', 19), ('Q', 33), ('N', 17), ('D', 20), ('S', 19), ('P', 21), ('O', 17), ('T', 19), ('Q', 30), ('N', 18), ('S', 20), ('P', 22), ('O', 18), ('R', 35), ('R', 32), ('T', 20), ('D', 21), ('R', 37), ('N', 19), ('S', 21), ('P', 23), ('D', 22), ('O', 19), ('T', 21), ('N', 20), ('S', 22), ('P', 24), ('Q', 32), ('O', 20), ('R', 34), ('Q', 37), ('T', 22), ('D', 23), ('Q', 35), ('D', 24), ('M', 32), ('N', 21), ('S', 23), ('P', 25), ('R', 39), ('O', 21), ('T', 23), ('N', 22), ('S', 24), ('P', 26), ('O', 22), ('T', 24), ('Q', 34), ('R', 36), ('D', 25), ('Q', 39), ('M', 33), ('D', 26), ('N', 23), ('R', 41), ('S', 25), ('P', 27), ('O', 23), ('T', 25), ('N', 24), ('S', 26), ('O', 24), ('Q', 36), ('R', 38), ('Q', 41), ('M', 34), ('D', 27), ('T', 26), ('R', 43), ('P', 28), ('N', 25), ('S', 27), ('Q', 38), ('O', 25), ('M', 35), ('N', 26), ('R', 40), ('D', 28), ('T', 27), ('R', 45), ('P', 29), ('R', 47), ('S', 28), ('M', 36), ('O', 26), ('N', 27), ('S', 29), ('D', 29), ('T', 28), ('O', 27), ('Q', 40), ('R', 42), ('P', 30), ('M', 37), ('D', 30), ('N', 28), ('T', 29), ('S', 30), ('Q', 42), ('O', 28), ('R', 44), ('P', 31), ('Q', 43), ('M', 38), ('D', 31), ('T', 30), ('A', 0), ('N', 29), ('S', 31), ('O', 29), ('A', 1), ('R', 46), ('M', 39), ('Q', 44), ('T', 31), ('A', 2), ('A', 3), ('Q', 45), ('M', 40), ('N', 30), ('N', 31), ('O', 30), ('Q', 46), ('M', 41), ('O', 31), ('Q', 47), ('M', 42), ('M', 43), ('M', 44), ('M', 45), ('M', 46), ('A', 4), ('M', 47), ('A', 5), ('A', 6), ('A', 7))
+TAIL_V = 4
+HEAD_S = (512, 384, 384, 512)
+TAIL_S = (512, 768)
+MID_S = 512
 
 
-def default_order():
-    order = []
-    n_pieces = 48
-    n_heads = 32
+def unit_list():
+    units = []
+    nv = 0
+    for n in range(N_QK):
+        units.extend([("q", n, 0), ("q", n, 1)])
+        if nv < 2 * N_V - TAIL_V:
+            units.append(("v", nv // 2, nv % 2))
+            nv += 1
+    while nv < 2 * N_V:
+        units.append(("v", nv // 2, nv % 2))
+        nv += 1
+    return units
 
-    def head(name, g):
-        if 0 <= g < n_heads:
-            order.append((name, g))
 
-    def piece(t):
-        order.append(("R", t))
-        m, nb = divmod(t, 2)
-        if nb == 1 and m >= 1 and m + RAW_BUFS < 24:
-            order.append(("L", m + RAW_BUFS))
-
-    for t in range(AHEAD):
-        piece(t)
-    for t in range(n_pieces + 12):
-        g = t - 8
-        head("N", g - L_NORM)
-        head("T", g - L_TURN)
-        head("P", g)
-        if t < n_pieces:
-            order.append(("Q", t))
-        head("D", g - L_TAB)
-        if t + AHEAD < n_pieces:
-            piece(t + AHEAD)
-        head("S", g - L_TAB)
-        head("O", g - L_OUT)
-        if t == T_PERF:
-            order.append(("f", 0))
-        if t == T_TABS:
-            order.append(("t", 0))
-        if t == T_VBIAS:
-            order.append(("v", 0))
-        if t == T_XT:
-            order.extend([("x", 0), ("x", 1)])
-        if t == T_XQ:
-            order.extend([("q", 0), ("q", 1)])
-        if 33 <= t <= n_pieces:
-            order.append(("M", t - 1))
-            if (t - 1) % 8 >= 6:
-                k = ((t - 1) // 8 - 4) * 4 + ((t - 1) % 2) * 2
-                order.extend([("A", k), ("A", k + 1)])
-    return order
+def scalar_columns(u, n_units):
+    if u < len(HEAD_S):
+        return HEAD_S[u]
+    if u >= n_units - len(TAIL_S):
+        return TAIL_S[u - (n_units - len(TAIL_S))]
+    return MID_S
 
 
 def tile_selfattention_pa_kernel(tc, x, pe, qkv_w, qkv_b, q_scale, k_scale, out_0, out_1, out_2):
     nc = tc.nc
     outs = (out_0, out_1, out_2)
+    units = unit_list()
+    n_units = len(units)
     with ExitStack() as ctx:
         ctx.enter_context(tc.manual_schedule())
         const = ctx.enter_context(tc.tile_pool(name="const", bufs=1))
-        rawp = ctx.enter_context(tc.tile_pool(name="rawp", bufs=RAW_BUFS))
-        grpp = ctx.enter_context(tc.tile_pool(name="grpp", bufs=6))
+        rawp = ctx.enter_context(tc.tile_pool(name="rawp", bufs=1))
+        grpp = ctx.enter_context(tc.tile_pool(name="grpp", bufs=GRP_BUFS))
         codp = ctx.enter_context(tc.tile_pool(name="codp", bufs=COD_BUFS))
-        dop = ctx.enter_context(tc.tile_pool(name="dop", bufs=4))
-        outp = ctx.enter_context(tc.tile_pool(name="outp", bufs=8))
-        smal = ctx.enter_context(tc.tile_pool(name="smal", bufs=4))
+        dop = ctx.enter_context(tc.tile_pool(name="dop", bufs=6))
+        outp = ctx.enter_context(tc.tile_pool(name="outp", bufs=6))
+        smal = ctx.enter_context(tc.tile_pool(name="smal", bufs=2))
         psum = ctx.enter_context(tc.psum_pool(name="psum", bufs=1))
 
-        n_loads = ROUNDS * PASSES
-        n_pieces = n_loads * 2
-        raws = {}
-        biases = {}
+        def load_key(kind, idx, c):
+            if kind == "q" and idx >= 2:
+                return ("f", idx // 2, c)
+            return ("h", kind, idx, c)
 
-        def load(m):
-            r, c = divmod(m, PASSES)
-            src = qkv_w[512 * c:512 * (c + 1), ROUNDW * r:ROUNDW * (r + 1)].rearrange("(p j) w -> p j w", j=4)
-            if m == 0:
-                for q in range(2):
-                    first = const.tile([P, 4, PIECE], BF16, name="first%d" % q)
-                    nc.sync.dma_start(out=first[:], in_=src[:, :, q * PIECE:(q + 1) * PIECE])
-                    raws[(m, q)] = first[:]
+        load_order = []
+        last_reader = {}
+        for u, (kind, idx, cp) in enumerate(units):
+            for c in (2 * cp, 2 * cp + 1):
+                key = load_key(kind, idx, c)
+                if key not in last_reader:
+                    load_order.append(key)
+                last_reader[key] = u
+        loaded = {}
+        issued = {"h": [], "f": []}
+        state = {"next_load": 0, "regrouped": -1}
+
+        def col0(kind, idx):
+            return BLK * idx if kind == "q" else BLK * (N_QK + idx)
+
+        def issue_load(key):
+            if key[0] == "f":
+                r, c = key[1], key[2]
+                rw = rawp.tile([P, 4, 2 * BLK], BF16, name="rf", tag="rf", bufs=FULL_BUFS)
+                src = qkv_w[512 * c:512 * (c + 1), 2 * BLK * r:2 * BLK * (r + 1)]
             else:
-                rw = rawp.tile([P, 4, ROUNDW], BF16, name="rw", tag="rw")
-                nc.sync.dma_start(out=rw[:], in_=src)
-                for q in range(2):
-                    raws[(m, q)] = rw[:, :, q * PIECE:(q + 1) * PIECE]
+                c = key[3]
+                lo = col0(key[1], key[2])
+                rw = rawp.tile([P, 4, BLK], BF16, name="rh", tag="rh", bufs=HALF_BUFS)
+                src = qkv_w[512 * c:512 * (c + 1), lo:lo + BLK]
+            nc.sync.dma_start(out=rw[:], in_=src.rearrange("(p j) w -> p j w", j=4))
+            loaded[key] = rw
+            issued[key[0]].append(key)
+
+        def loads(limit=None):
+            n = 0
+            while state["next_load"] < len(load_order) and (limit is None or n < limit):
+                key = load_order[state["next_load"]]
+                done = issued[key[0]]
+                bufs = FULL_BUFS if key[0] == "f" else HALF_BUFS
+                if len(done) >= bufs and last_reader[done[len(done) - bufs]] > state["regrouped"]:
+                    break
+                issue_load(key)
+                state["next_load"] += 1
+                n += 1
+
+        def raw_piece(kind, idx, c):
+            key = load_key(kind, idx, c)
+            if key[0] == "f":
+                nb = idx % 2
+                return loaded[key][:, :, BLK * nb:BLK * (nb + 1)]
+            return loaded[key][:]
 
         ident = const.tile([P, P], F32, name="ident")
         make_identity(nc, ident[:])
@@ -134,31 +145,30 @@ def tile_selfattention_pa_kernel(tc, x, pe, qkv_w, qkv_b, q_scale, k_scale, out_
         nc.gpsimd.tensor_copy(out=swp[:, :, 1], in_=idv[:, :, 0])
         eps = const.tile([P, 1], F32, name="eps")
         nc.vector.memset(eps[:], EPS)
-        ones = const.tile([P, P], F32, name="ones")
+        ones = const.tile([P, SS_N], F32, name="ones")
         nc.vector.memset(ones[:], 1.0)
         hrows = const.tile([P, P], BF16, name="hrows")
         nc.vector.memset(hrows[:].bitcast(I32), 0)
-        vrows = const.tile([P, PIECE], BF16, name="vrows")
+        vrows = const.tile([P, BLK], BF16, name="vrows")
         nc.vector.memset(vrows[:].bitcast(I32), 0)
 
-        load(0)
+        loads(2)
         nc.sync.dma_start(out=hrows[0:32, :], in_=qkv_b[0:4096].rearrange("(j n) -> j n", n=HD))
         nc.sync.dma_start(out=hrows[32:33, :], in_=q_scale.rearrange("(o n) -> o n", o=1))
         nc.sync.dma_start(out=hrows[33:34, :], in_=k_scale.rearrange("(o n) -> o n", o=1))
         pe_sb = const.tile([P, 256], BF16, name="pe_sb")
         nc.sync.dma_start(out=pe_sb[:], in_=pe.rearrange("a b l i r c -> (a b l) (i r c)"))
-        load(1)
+        loads(2)
         x_sb = const.tile([P, B, DIM], BF16, name="x_sb")
         for b in range(B):
             nc.sync.dma_start(out=x_sb[:, b, :], in_=x[b])
-        nc.sync.dma_start(out=vrows[0:4, :], in_=qkv_b[4096:6144].rearrange("(j n) -> j n", n=PIECE))
-        for m in range(2, RAW_BUFS + 1):
-            load(m)
+        nc.sync.dma_start(out=vrows[0:4, :], in_=qkv_b[4096:6144].rearrange("(j n) -> j n", n=BLK))
+        loads()
 
         per_f = const.tile([P, 34], F32, name="per_f")
         pel = const.tile([P, 2, 64, 2], F32, name="pel")
         tabs = []
-        setup = {}
+        bias_v = const.tile([P, N_V * BLK], BF16, name="bias_v")
 
         def per_feature():
             hps = psum.tile([P, P], BF16, name="hps", tag="rb", bufs=2)
@@ -181,13 +191,11 @@ def tile_selfattention_pa_kernel(tc, x, pe, qkv_w, qkv_b, q_scale, k_scale, out_
 
         def v_bias():
             for i in range(2):
-                bank = psum.tile([P, 2, PIECE], BF16, name="bank", tag="pt", bufs=2)
+                bank = psum.tile([P, 2, BLK], BF16, name="bank", tag="pt", bufs=PT_BUFS)
                 for h in range(2):
                     j = 2 * i + h
                     nc.tensor.matmul(out=bank[:, h, :], lhsT=identb[:, j:j + 1].to_broadcast([P, P]), rhs=vrows[:], start=True, stop=True)
-                b_sb = const.tile([P, ROUNDW], BF16, name="b_sb%d" % i)
-                nc.scalar.copy(out=b_sb[:], in_=bank[:].rearrange("p h n -> p (h n)"))
-                biases[QK_ROUNDS + i] = b_sb
+                nc.scalar.copy(out=bias_v[:, 2 * BLK * i:2 * BLK * (i + 1)], in_=bank[:].rearrange("p h n -> p (h n)"))
 
         xw = x_sb[:].bitcast(F32)
         xg = const.tile([P, 4 * B * P * PASSES], BF16, name="xg", align_bytes=64)
@@ -197,7 +205,10 @@ def tile_selfattention_pa_kernel(tc, x, pe, qkv_w, qkv_b, q_scale, k_scale, out_
 
         def x_turn(cp):
             for b in range(B):
-                xt = psum.tile([P, 2, 2, P], F32, name="xt", tag="va%d%d" % (b, cp))
+                if b == 0:
+                    xt = psum.tile([P, 2, 2, P], F32, name="xt", tag="va", bufs=2)
+                else:
+                    xt = psum.tile([P, 2, 2, P], F32, name="xt", tag="pt", bufs=PT_BUFS)
                 for c2 in range(2):
                     c = 2 * cp + c2
                     for u in range(2):
@@ -213,136 +224,197 @@ def tile_selfattention_pa_kernel(tc, x, pe, qkv_w, qkv_b, q_scale, k_scale, out_
 
         grps = {}
         cods = {}
-        accs = {}
-        agenda = {}
+        live = {}
+        ready = {}
+        for u, (kind, idx, cp) in enumerate(units):
+            if cp == 1:
+                ready[(kind, idx)] = u
+        burst_slots = [ready[("q", n)] + LAG_D for n in range(N_QK)]
 
-        def later(t, job):
-            agenda[t] = agenda.get(t, []) + [job]
+        def grp_tile(u):
+            if u not in grps:
+                if POOL_COLS > 0 and u in burst_slots:
+                    grps[u] = grpp.tile([P, 2, BLK, 4], BF16, name="grpg", tag="grpg", bufs=1, align_bytes=64)
+                else:
+                    grps[u] = grpp.tile([P, 2, BLK, 4], BF16, name="grp", tag="grp", align_bytes=64)
+            return grps[u]
 
-        def where(t):
-            m, nb = divmod(t, 2)
-            r, c = divmod(m, PASSES)
-            return m, r, c, nb
+        def regroup(engine, u, lo, hi):
+            if lo < BLK < hi:
+                regroup(engine, u, lo, BLK)
+                regroup(engine, u, BLK, hi)
+            elif lo < hi:
+                regroup_piece(engine, u, lo // BLK, lo % BLK, hi - BLK * (lo // BLK))
 
-        def regroup(t):
-            m, r, c, nb = where(t)
-            grp = grpp.tile([P, PIECE, 4], BF16, name="grp", tag="grp", align_bytes=64)
-            src = raws[(m, nb)].rearrange("p t (c i) -> p c t i", i=4)
-            dst = grp[:].rearrange("p (c i) t -> p c t i", i=4)
-            if SHARE[r][c * 2 + nb] == "V":
+        def regroup_piece(engine, u, c2, lo, hi):
+            kind, idx, cp = units[u]
+            src = raw_piece(kind, idx, 2 * cp + c2)[:, :, lo:hi].rearrange("p t (c i) -> p c t i", i=4)
+            dst = grp_tile(u)[:, c2, lo:hi, :].rearrange("p (c i) t -> p c t i", i=4)
+            if engine == "V":
                 nc.vector.tensor_copy(out=dst, in_=src)
-            else:
+            elif engine == "S":
                 nc.scalar.copy(out=dst, in_=src)
-            grps[t] = grp
+            else:
+                nc.gpsimd.tensor_scalar(out=dst, in0=src, scalar1=1.0, scalar2=0.0, op0=ALU.mult, op1=ALU.add)
 
-        def quantise(t):
-            m, r, c, nb = where(t)
-            cod = codp.tile([P, PIECE], U32, name="cod", tag="cod", align_bytes=64)
-            scl = codp.tile([P, PIECE], U8, name="scl", tag="scl", align_bytes=64)
-            nc.vector.quantize_mx(out=cod[:].bitcast(FP8X4), scales=scl[:], in_=grps[t][:].rearrange("p w t -> p (w t)"))
-            cods[(r, c, nb)] = (cod, scl)
+        def regroup_s(u):
+            regroup("S", u, 0, scalar_columns(u, n_units))
 
-        def store(r, b, nb, o_t):
-            h0 = (r % 2) * 8 + nb * 4
+        def pool_columns(u):
+            if u in burst_slots[1:]:
+                return POOL_COLS
+            return 0
+
+        def regroup_g(u):
+            regroup("G", u, 2 * BLK - pool_columns(u), 2 * BLK)
+
+        def regroup_v(u):
+            regroup("V", u, scalar_columns(u, n_units), 2 * BLK - pool_columns(u))
+            state["regrouped"] = u
+
+        def quantise(u):
+            cod = codp.tile([P, 2 * BLK], U32, name="cod", tag="cod", align_bytes=64)
+            scl = codp.tile([P, 2 * BLK], U8, name="scl", tag="scl", align_bytes=64)
+            nc.vector.quantize_mx(out=cod[:].bitcast(FP8X4), scales=scl[:], in_=grps[u][:].rearrange("p a w t -> p (a w t)"))
+            cods[units[u]] = (cod, scl)
+
+        def store(s, b, h0, o_t):
             nc.sync.dma_start(
-                out=outs[r // 2][b, h0:h0 + 4, :, :].rearrange("h l d -> l h d"),
+                out=outs[s][b, h0:h0 + 4, :, :].rearrange("h l d -> l h d"),
                 in_=o_t[:].rearrange("p (h d) -> p h d", h=4),
             )
 
-        live = {}
+        def project(n):
+            for k in range(2):
+                pt = psum.tile([P, 2, TOK], F32, name="pt", tag="pt", bufs=PT_BUFS)
+                live[("pt", n, k)] = pt
+                for hh in range(2):
+                    j = 2 * k + hh
+                    for c in range(PASSES):
+                        cod, scl = cods[("q", n, c // 2)]
+                        lo = (c % 2) * BLK + j * HD
+                        nc.tensor.matmul_mx(
+                            out=pt[:, hh, :],
+                            lhsT=cod[:, lo:lo + HD].bitcast(FP8X4),
+                            lhsT_scale=scl[:, lo:lo + HD],
+                            rhs=xq[:, TOK * c:TOK * (c + 1)].bitcast(FP8X4),
+                            rhs_scale=xs[:, TOK * c:TOK * (c + 1)],
+                            start=(c == 0),
+                            stop=(c == PASSES - 1),
+                        )
 
-        def head_project(g):
-            r, j = divmod(g, 8)
-            nb, hh = divmod(j, 4)
-            pt = psum.tile([P, TOK], F32, name="pt", tag="pt", bufs=2)
-            live[("pt", g)] = pt
-            for c in range(PASSES):
-                cod, scl = cods[(r, c, nb)]
-                nc.tensor.matmul_mx(
-                    out=pt[:],
-                    lhsT=cod[:, hh * HD:(hh + 1) * HD].bitcast(FP8X4),
-                    lhsT_scale=scl[:, hh * HD:(hh + 1) * HD],
-                    rhs=xq[:, TOK * c:TOK * (c + 1)].bitcast(FP8X4),
-                    rhs_scale=xs[:, TOK * c:TOK * (c + 1)],
-                    start=(c == 0),
-                    stop=(c == PASSES - 1),
+        def tables_times(n):
+            for j in range(4):
+                g = 4 * n + j
+                do = dop.tile([P, 2, TOK], F32, name="do", tag="do")
+                nc.vector.scalar_tensor_tensor(
+                    out=do[:],
+                    in0=live[("pt", n, j // 2)][:, j % 2, :].unsqueeze(1).to_broadcast([P, 2, TOK]),
+                    scalar=per_f[:, g:g + 1],
+                    in1=tabs[g // 16][:].rearrange("p d b l -> p d (b l)"),
+                    op0=ALU.add,
+                    op1=ALU.mult,
                 )
+                live[("do", g)] = do
 
-        def head_tables(g):
-            pt = live[("pt", g)]
-            do = dop.tile([P, 2, TOK], F32, name="do", tag="do")
-            nc.vector.scalar_tensor_tensor(
-                out=do[:],
-                in0=pt[:].unsqueeze(1).to_broadcast([P, 2, TOK]),
-                scalar=per_f[:, g:g + 1],
-                in1=tabs[g // 16][:].rearrange("p d b l -> p d (b l)"),
-                op0=ALU.add,
-                op1=ALU.mult,
-            )
-            live[("do", g)] = do
+        def squares(n):
+            for j in range(4):
+                g = 4 * n + j
+                sq = dop.tile([P, TOK], F32, name="sq", tag="sq")
+                nc.scalar.activation(out=sq[:], in_=live[("pt", n, j // 2)][:, j % 2, :], func=ACT.Square, bias=per_f[:, g:g + 1], scale=1.0)
+                live[("sq", g)] = sq
 
-        def head_squares(g):
-            pt = live[("pt", g)]
-            sq = dop.tile([P, TOK], F32, name="sq", tag="sq")
-            nc.scalar.activation(out=sq[:], in_=pt[:], func=ACT.Square, bias=per_f[:, g:g + 1], scale=1.0)
-            live[("sq", g)] = sq
+        def turn(n):
+            ssb = psum.tile([P, 8, SS_N], F32, name="ssb", tag="ss", bufs=1)
+            live[("ss", n)] = ssb
+            for k in range(2):
+                rb = psum.tile([P, 2, B, P], F32, name="rb", tag="rb", bufs=2)
+                live[("rb", n, k)] = rb
+                for hh in range(2):
+                    j = 2 * k + hh
+                    g = 4 * n + j
+                    for b in range(B):
+                        nc.tensor.matmul(out=ssb[:, 2 * j + b, :], lhsT=live[("sq", g)][:, P * b:P * (b + 1)], rhs=ones[:], start=True, stop=True)
+                    for b in range(B):
+                        tok = slice(P * b, P * (b + 1))
+                        nc.tensor.matmul(out=rb[:, hh, b, :], lhsT=live[("do", g)][:, 0, tok], rhs=ident[:], is_transpose=True, start=True, stop=False)
+                        nc.tensor.matmul(out=rb[:, hh, b, :], lhsT=live[("do", g)][:, 1, tok], rhs=swp[:].rearrange("p i c -> p (i c)"), is_transpose=True, start=False, stop=True)
 
-        def head_turn(g):
-            rb = psum.tile([P, 4, P], F32, name="rb", tag="rb", bufs=2)
+        def norm_out(n):
+            rr = smal.tile([P, 8], F32, name="rr", tag="rr")
+            nc.scalar.activation(out=rr[:], in_=live[("ss", n)][:, :, 0], func=ACT.Abs_reciprocal_sqrt, bias=eps[:], scale=1.0 / HD)
+            o_ts = []
             for b in range(B):
-                nc.tensor.matmul(out=rb[:, 2 + b, :], lhsT=live[("sq", g)][:, P * b:P * (b + 1)], rhs=ones[:], start=True, stop=True)
+                o_t = outp.tile([P, BLK], F32, name="o_t", tag="o_t")
+                o_ts.append(o_t)
+            for j in range(4):
+                for b in range(B):
+                    nc.scalar.activation(out=o_ts[b][:, j * HD:(j + 1) * HD], in_=live[("rb", n, j // 2)][:, j % 2, b, :], func=ACT.Copy, scale=rr[:, 2 * j + b:2 * j + b + 1])
             for b in range(B):
-                tok = slice(P * b, P * (b + 1))
-                nc.tensor.matmul(out=rb[:, b, :], lhsT=live[("do", g)][:, 0, tok], rhs=ident[:], is_transpose=True, start=True, stop=False)
-                nc.tensor.matmul(out=rb[:, b, :], lhsT=live[("do", g)][:, 1, tok], rhs=swp[:].rearrange("p i c -> p (i c)"), is_transpose=True, start=False, stop=True)
-            live[("rb", g)] = rb
+                store(n // 4, b, (n % 4) * 4, o_ts[b])
 
-        def head_norm(g):
-            rr = smal.tile([P, 2], F32, name="rr", tag="rr")
-            nc.scalar.activation(out=rr[:], in_=live[("rb", g)][:, 2:4, 0], func=ACT.Abs_reciprocal_sqrt, bias=eps[:], scale=1.0 / HD)
-            live[("rr", g)] = rr
+        def multiply(u):
+            kind, j, cp = units[u]
+            cod, scl = cods[units[u]]
+            for c2 in range(2):
+                c = 2 * cp + c2
+                for b in range(B):
+                    if c == 0:
+                        live[("acc", j, b)] = psum.tile([P, BLK], F32, name="acc", tag="va", bufs=2)
+                    lo = (c * B + b) * P
+                    nc.tensor.matmul_mx(
+                        out=live[("acc", j, b)][:],
+                        lhsT=xq[:, lo:lo + P].bitcast(FP8X4),
+                        lhsT_scale=xs[:, lo:lo + P],
+                        rhs=cod[:, c2 * BLK:(c2 + 1) * BLK].bitcast(FP8X4),
+                        rhs_scale=scl[:, c2 * BLK:(c2 + 1) * BLK],
+                        start=(c == 0),
+                        stop=(c == PASSES - 1),
+                    )
 
-        def head_out(g):
-            r, j = divmod(g, 8)
-            nb, hh = divmod(j, 4)
+        def add_bias(j):
             for b in range(B):
-                if hh == 0:
-                    live[("o", g // 4, b)] = outp.tile([P, PIECE], F32, name="o_t", tag="o_t")
-                o_t = live[("o", g // 4, b)]
-                nc.scalar.activation(out=o_t[:, hh * HD:(hh + 1) * HD], in_=live[("rb", g)][:, b, :], func=ACT.Copy, scale=live[("rr", g)][:, b:b + 1])
-                if hh == 3:
-                    store(r, b, nb, o_t)
+                o_t = outp.tile([P, BLK], F32, name="o_t", tag="o_t")
+                nc.vector.tensor_tensor(out=o_t[:], in0=live[("acc", j, b)][:], in1=bias_v[:, BLK * j:BLK * (j + 1)], op=ALU.add)
+                store(2, b, 4 * j, o_t)
 
-        def add_bias(k):
-            r, rest = divmod(k, 4)
-            nb, b = divmod(rest, 2)
-            r += QK_ROUNDS
-            o_t = outp.tile([P, PIECE], F32, name="o_t", tag="o_t")
-            nc.vector.tensor_tensor(out=o_t[:], in0=accs[(b, nb)][:], in1=biases[r][:, PIECE * nb:PIECE * (nb + 1)], op=ALU.add)
-            store(r, b, nb, o_t)
-
-        def multiply(t):
-            m, r, c, nb = where(t)
-            cod, scl = cods[(r, c, nb)]
-            for b in range(B):
-                if c == 0:
-                    accs[(b, nb)] = psum.tile([P, PIECE], F32, name="acc", tag="va%d%d" % (b, nb))
-                lo = (c * B + b) * P
-                nc.tensor.matmul_mx(
-                    out=accs[(b, nb)][:],
-                    lhsT=xq[:, lo:lo + P].bitcast(FP8X4),
-                    lhsT_scale=xs[:, lo:lo + P],
-                    rhs=cod[:].bitcast(FP8X4),
-                    rhs_scale=scl[:],
-                    start=(c == 0),
-                    stop=(c == PASSES - 1),
-                )
-
-        steps = {
-            "L": load, "R": regroup, "Q": quantise, "P": head_project, "D": head_tables, "S": head_squares,
-            "T": head_turn, "N": head_norm, "O": head_out, "M": multiply, "A": add_bias,
-            "f": lambda k: per_feature(), "t": lambda k: tables(), "v": lambda k: v_bias(), "x": x_turn, "q": x_quantise,
-        }
-        for name, k in ORDER or default_order():
-            MARK.append((name, k))
-            steps[name](k)
+        for u in range(AHEAD_S):
+            regroup_s(u)
+            if u < AHEAD_V:
+                regroup_v(u)
+        per_feature()
+        tables()
+        for cp in range(2):
+            x_turn(cp)
+        v_bias()
+        for k in range(n_units + LAG_O + 1):
+            if k + AHEAD_S < n_units:
+                regroup_s(k + AHEAD_S)
+            if k + AHEAD_V < n_units:
+                regroup_v(k + AHEAD_V)
+            loads()
+            if k < n_units:
+                quantise(k)
+            if k == 0:
+                for cp in range(2):
+                    x_quantise(cp)
+            for n in range(N_QK):
+                if ready[("q", n)] + LAG_O == k:
+                    norm_out(n)
+            for j in range(N_V):
+                if ready[("v", j)] + 1 == k:
+                    add_bias(j)
+            for n in range(N_QK):
+                if ready[("q", n)] == k:
+                    project(n)
+            if k < n_units and units[k][0] == "v":
+                multiply(k)
+            for n in range(N_QK):
+                if ready[("q", n)] + LAG_D == k:
+                    if n + 1 < N_QK:
+                        regroup_g(burst_slots[n + 1])
+                    tables_times(n)
+            for n in range(N_QK):
+                if ready[("q", n)] + LAG_SQ == k:
+                    squares(n)
+                    turn(n)

@@ -34,14 +34,16 @@ AHEAD_V = 1
 LAG_D = 1
 LAG_SQ = 1
 LAG_O = 3
-POOL_COLS = 0
+POOL_COLS = 384
 PT_BUFS = 3
+POOL_FIRST = 0
+POOL_AHEAD = 2
 
 
 TAIL_V = 4
 HEAD_S = (512, 384, 384, 512)
 TAIL_S = (512, 768)
-MID_S = 512
+MID_S = 464
 
 
 def unit_list():
@@ -233,10 +235,7 @@ def tile_selfattention_pa_kernel(tc, x, pe, qkv_w, qkv_b, q_scale, k_scale, out_
 
         def grp_tile(u):
             if u not in grps:
-                if POOL_COLS > 0 and u in burst_slots:
-                    grps[u] = grpp.tile([P, 2, BLK, 4], BF16, name="grpg", tag="grpg", bufs=1, align_bytes=64)
-                else:
-                    grps[u] = grpp.tile([P, 2, BLK, 4], BF16, name="grp", tag="grp", align_bytes=64)
+                grps[u] = grpp.tile([P, 2, BLK, 4], BF16, name="grp", tag="grp", align_bytes=64)
             return grps[u]
 
         def regroup(engine, u, lo, hi):
@@ -255,18 +254,23 @@ def tile_selfattention_pa_kernel(tc, x, pe, qkv_w, qkv_b, q_scale, k_scale, out_
             elif engine == "S":
                 nc.scalar.copy(out=dst, in_=src)
             else:
-                nc.gpsimd.tensor_scalar(out=dst, in0=src, scalar1=1.0, scalar2=0.0, op0=ALU.mult, op1=ALU.add)
+                src = raw_piece(kind, idx, 2 * cp + c2)[:, :, lo:hi].rearrange("p t w -> p w t")
+                dst = grp_tile(u)[:, c2, lo:hi, :]
+                nc.gpsimd.tensor_scalar(out=dst, in0=src, scalar1=live["gate"][:, 0:1], scalar2=0.0, op0=ALU.mult, op1=ALU.add)
 
         def regroup_s(u):
             regroup("S", u, 0, scalar_columns(u, n_units))
 
         def pool_columns(u):
-            if u in burst_slots[1:]:
+            if u < n_units and u - POOL_AHEAD in burst_slots[POOL_FIRST:]:
                 return POOL_COLS
             return 0
 
         def regroup_g(u):
-            regroup("G", u, 2 * BLK - pool_columns(u), 2 * BLK)
+            if pool_columns(u) > 0:
+                live["gate"] = smal.tile([P, 1], F32, name="gate", tag="gate")
+                nc.vector.memset(live["gate"][:], 1.0)
+                regroup("G", u, 2 * BLK - pool_columns(u), 2 * BLK)
 
         def regroup_v(u):
             regroup("V", u, scalar_columns(u, n_units), 2 * BLK - pool_columns(u))
@@ -411,8 +415,7 @@ def tile_selfattention_pa_kernel(tc, x, pe, qkv_w, qkv_b, q_scale, k_scale, out_
                 multiply(k)
             for n in range(N_QK):
                 if ready[("q", n)] + LAG_D == k:
-                    if n + 1 < N_QK:
-                        regroup_g(burst_slots[n + 1])
+                    regroup_g(k + POOL_AHEAD)
                     tables_times(n)
             for n in range(N_QK):
                 if ready[("q", n)] + LAG_SQ == k:

@@ -34,6 +34,7 @@ AHEAD_V = 1
 LAG_D = 1
 LAG_SQ = 1
 LAG_O = 3
+RUN = 8
 POOL_COLS = 384
 PT_BUFS = 3
 POOL_FIRST = 0
@@ -247,8 +248,8 @@ def tile_selfattention_pa_kernel(tc, x, pe, qkv_w, qkv_b, q_scale, k_scale, out_
 
         def regroup_piece(engine, u, c2, lo, hi):
             kind, idx, cp = units[u]
-            src = raw_piece(kind, idx, 2 * cp + c2)[:, :, lo:hi].rearrange("p t (c i) -> p c t i", i=4)
-            dst = grp_tile(u)[:, c2, lo:hi, :].rearrange("p (c i) t -> p c t i", i=4)
+            src = raw_piece(kind, idx, 2 * cp + c2)[:, :, lo:hi].rearrange("p t (c i) -> p c t i", i=RUN)
+            dst = grp_tile(u)[:, c2, lo:hi, :].rearrange("p (c i) t -> p c t i", i=RUN)
             if engine == "V":
                 nc.vector.tensor_copy(out=dst, in_=src)
             elif engine == "S":

@@ -18,55 +18,44 @@ DIM = 2048
 HD = 128
 PASSES = 4
 BLK = 512
+GW = 1024
 TOK = B * P
 EPS = 1e-6
 FLOPS = 2 * 256 * 2048 * 6144
 
-N_QK = 8
-N_V = 4
+N_QK = 4
+N_V = 2
+N_PAIR = 16
 SS_N = 64
-HALF_BUFS = 8
-FULL_BUFS = 6
+RAW_BUFS = 9
 GRP_BUFS = 4
-COD_BUFS = 8
+COD_BUFS = 9
+DO_BUFS = 3
+OUT_BUFS = 5
 AHEAD_S = 2
 AHEAD_V = 1
-LAG_D = 1
-LAG_SQ = 1
-LAG_O = 3
+FIRST_PAIR = 4
+LAG_O = 1
 RUN = 8
-POOL_COLS = 384
-PT_BUFS = 3
-POOL_FIRST = 0
+POOL_COLS = 192
 POOL_AHEAD = 2
-
-
-TAIL_V = 4
-HEAD_S = (512, 384, 384, 512)
-TAIL_S = (512, 768)
-MID_S = 464
+S_HEAD = (512, 448, 448, 448)
+S_PAIR = 448
+S_V = 512
+S_TAIL = 608
+X_STEP = (1, 2)
+VB_STEP = 2
 
 
 def unit_list():
     units = []
-    nv = 0
     for n in range(N_QK):
-        units.extend([("q", n, 0), ("q", n, 1)])
-        if nv < 2 * N_V - TAIL_V:
-            units.append(("v", nv // 2, nv % 2))
-            nv += 1
-    while nv < 2 * N_V:
-        units.append(("v", nv // 2, nv % 2))
-        nv += 1
+        for c in range(PASSES):
+            units.append(("q", n, c))
+    for j in range(2 * N_V):
+        for cp in range(2):
+            units.append(("v", j, cp))
     return units
-
-
-def scalar_columns(u, n_units):
-    if u < len(HEAD_S):
-        return HEAD_S[u]
-    if u >= n_units - len(TAIL_S):
-        return TAIL_S[u - (n_units - len(TAIL_S))]
-    return MID_S
 
 
 def tile_selfattention_pa_kernel(tc, x, pe, qkv_w, qkv_b, q_scale, k_scale, out_0, out_1, out_2):
@@ -80,63 +69,51 @@ def tile_selfattention_pa_kernel(tc, x, pe, qkv_w, qkv_b, q_scale, k_scale, out_
         rawp = ctx.enter_context(tc.tile_pool(name="rawp", bufs=1))
         grpp = ctx.enter_context(tc.tile_pool(name="grpp", bufs=GRP_BUFS))
         codp = ctx.enter_context(tc.tile_pool(name="codp", bufs=COD_BUFS))
-        dop = ctx.enter_context(tc.tile_pool(name="dop", bufs=6))
-        outp = ctx.enter_context(tc.tile_pool(name="outp", bufs=6))
-        smal = ctx.enter_context(tc.tile_pool(name="smal", bufs=2))
+        dop = ctx.enter_context(tc.tile_pool(name="dop", bufs=DO_BUFS))
+        outp = ctx.enter_context(tc.tile_pool(name="outp", bufs=OUT_BUFS))
+        smal = ctx.enter_context(tc.tile_pool(name="smal", bufs=3))
         psum = ctx.enter_context(tc.psum_pool(name="psum", bufs=1))
-
-        def load_key(kind, idx, c):
-            if kind == "q" and idx >= 2:
-                return ("f", idx // 2, c)
-            return ("h", kind, idx, c)
 
         load_order = []
         last_reader = {}
-        for u, (kind, idx, cp) in enumerate(units):
-            for c in (2 * cp, 2 * cp + 1):
-                key = load_key(kind, idx, c)
+        for u, (kind, idx, c) in enumerate(units):
+            if kind == "q":
+                keys = [("q", idx, c)]
+            else:
+                keys = [("v", idx // 2, 2 * c), ("v", idx // 2, 2 * c + 1)]
+            for key in keys:
                 if key not in last_reader:
                     load_order.append(key)
                 last_reader[key] = u
         loaded = {}
-        issued = {"h": [], "f": []}
         state = {"next_load": 0, "regrouped": -1}
 
-        def col0(kind, idx):
-            return BLK * idx if kind == "q" else BLK * (N_QK + idx)
-
-        def issue_load(key):
-            if key[0] == "f":
-                r, c = key[1], key[2]
-                rw = rawp.tile([P, 4, 2 * BLK], BF16, name="rf", tag="rf", bufs=FULL_BUFS)
-                src = qkv_w[512 * c:512 * (c + 1), 2 * BLK * r:2 * BLK * (r + 1)]
-            else:
-                c = key[3]
-                lo = col0(key[1], key[2])
-                rw = rawp.tile([P, 4, BLK], BF16, name="rh", tag="rh", bufs=HALF_BUFS)
-                src = qkv_w[512 * c:512 * (c + 1), lo:lo + BLK]
-            nc.sync.dma_start(out=rw[:], in_=src.rearrange("(p j) w -> p j w", j=4))
+        def issue_load(key, pieces):
+            kind, idx, c = key
+            lo = GW * idx if kind == "q" else GW * (N_QK + idx)
+            rw = rawp.tile([P, 4, GW], BF16, name="raw", tag="raw", bufs=RAW_BUFS)
+            w = GW // pieces
+            for i in range(pieces):
+                src = qkv_w[512 * c:512 * (c + 1), lo + w * i:lo + w * (i + 1)]
+                nc.sync.dma_start(out=rw[:, :, w * i:w * (i + 1)], in_=src.rearrange("(p j) w -> p j w", j=4))
             loaded[key] = rw
-            issued[key[0]].append(key)
 
-        def loads(limit=None):
+        def loads(limit=None, pieces=1):
             n = 0
             while state["next_load"] < len(load_order) and (limit is None or n < limit):
-                key = load_order[state["next_load"]]
-                done = issued[key[0]]
-                bufs = FULL_BUFS if key[0] == "f" else HALF_BUFS
-                if len(done) >= bufs and last_reader[done[len(done) - bufs]] > state["regrouped"]:
+                i = state["next_load"]
+                if i >= RAW_BUFS and last_reader[load_order[i - RAW_BUFS]] > state["regrouped"]:
                     break
-                issue_load(key)
+                issue_load(load_order[i], pieces)
                 state["next_load"] += 1
                 n += 1
 
-        def raw_piece(kind, idx, c):
-            key = load_key(kind, idx, c)
-            if key[0] == "f":
-                nb = idx % 2
-                return loaded[key][:, :, BLK * nb:BLK * (nb + 1)]
-            return loaded[key][:]
+        def raw_piece(u, half):
+            kind, idx, c = units[u]
+            if kind == "q":
+                return loaded[units[u]][:, :, BLK * half:BLK * (half + 1)]
+            j = idx % 2
+            return loaded[("v", idx // 2, 2 * c + half)][:, :, BLK * j:BLK * (j + 1)]
 
         ident = const.tile([P, P], F32, name="ident")
         make_identity(nc, ident[:])
@@ -155,13 +132,13 @@ def tile_selfattention_pa_kernel(tc, x, pe, qkv_w, qkv_b, q_scale, k_scale, out_
         vrows = const.tile([P, BLK], BF16, name="vrows")
         nc.vector.memset(vrows[:].bitcast(I32), 0)
 
-        loads(2)
+        loads(1, 2)
         nc.sync.dma_start(out=hrows[0:32, :], in_=qkv_b[0:4096].rearrange("(j n) -> j n", n=HD))
         nc.sync.dma_start(out=hrows[32:33, :], in_=q_scale.rearrange("(o n) -> o n", o=1))
         nc.sync.dma_start(out=hrows[33:34, :], in_=k_scale.rearrange("(o n) -> o n", o=1))
         pe_sb = const.tile([P, 256], BF16, name="pe_sb")
         nc.sync.dma_start(out=pe_sb[:], in_=pe.rearrange("a b l i r c -> (a b l) (i r c)"))
-        loads(2)
+        loads(1)
         x_sb = const.tile([P, B, DIM], BF16, name="x_sb")
         for b in range(B):
             nc.sync.dma_start(out=x_sb[:, b, :], in_=x[b])
@@ -171,7 +148,7 @@ def tile_selfattention_pa_kernel(tc, x, pe, qkv_w, qkv_b, q_scale, k_scale, out_
         per_f = const.tile([P, 34], F32, name="per_f")
         pel = const.tile([P, 2, 64, 2], F32, name="pel")
         tabs = []
-        bias_v = const.tile([P, N_V * BLK], BF16, name="bias_v")
+        bias_v = const.tile([P, 2 * N_V * BLK], BF16, name="bias_v")
 
         def per_feature():
             hps = psum.tile([P, P], BF16, name="hps", tag="rb", bufs=2)
@@ -187,14 +164,14 @@ def tile_selfattention_pa_kernel(tc, x, pe, qkv_w, qkv_b, q_scale, k_scale, out_
             for d in range(2):
                 nc.tensor.transpose(tps[:, d, :], pel[:, d, :, :].rearrange("p i c -> p (i c)"), ident[:])
             for s in range(2):
-                tab = const.tile([P, 2, B, P], F32, name="tab%d" % s)
+                tab = const.tile([P, 2, 2, B, 64], F32, name="tab%d" % s)
                 for b in range(B):
-                    nc.scalar.activation(out=tab[:, :, b, :], in_=tps[:], func=ACT.Copy, scale=per_f[:, 32 + s:33 + s])
+                    nc.scalar.activation(out=tab[:, :, :, b, :], in_=tps[:].rearrange("p d (i e) -> p d e i", e=2), func=ACT.Copy, scale=per_f[:, 32 + s:33 + s])
                 tabs.append(tab)
 
         def v_bias():
             for i in range(2):
-                bank = psum.tile([P, 2, BLK], BF16, name="bank", tag="pt", bufs=PT_BUFS)
+                bank = psum.tile([P, 2, BLK], BF16, name="bank", tag="va", bufs=2)
                 for h in range(2):
                     j = 2 * i + h
                     nc.tensor.matmul(out=bank[:, h, :], lhsT=identb[:, j:j + 1].to_broadcast([P, P]), rhs=vrows[:], start=True, stop=True)
@@ -206,12 +183,16 @@ def tile_selfattention_pa_kernel(tc, x, pe, qkv_w, qkv_b, q_scale, k_scale, out_
         xq = const.tile([P, PASSES * B * P], U32, name="xq", align_bytes=64)
         xs = const.tile([P, PASSES * B * P], U8, name="xs", align_bytes=64)
 
+        xqp = const.tile([P, PASSES, 2, B, 64], U32, name="xqp", align_bytes=64)
+        xsp = const.tile([P, PASSES, 2, B, 64], U8, name="xsp", align_bytes=64)
+
+        def x_by_parity():
+            nc.vector.tensor_copy(out=xqp[:], in_=xq[:].rearrange("p (c b i e) -> p c e b i", c=PASSES, b=B, e=2))
+            nc.vector.tensor_copy(out=xsp[:], in_=xs[:].rearrange("p (c b i e) -> p c e b i", c=PASSES, b=B, e=2))
+
         def x_turn(cp):
             for b in range(B):
-                if b == 0:
-                    xt = psum.tile([P, 2, 2, P], F32, name="xt", tag="va", bufs=2)
-                else:
-                    xt = psum.tile([P, 2, 2, P], F32, name="xt", tag="pt", bufs=PT_BUFS)
+                xt = psum.tile([P, 2, 2, P], F32, name="xt", tag="va" if b == 0 else "pt", bufs=2 if b == 0 else 3)
                 for c2 in range(2):
                     c = 2 * cp + c2
                     for u in range(2):
@@ -228,135 +209,132 @@ def tile_selfattention_pa_kernel(tc, x, pe, qkv_w, qkv_b, q_scale, k_scale, out_
         grps = {}
         cods = {}
         live = {}
-        ready = {}
-        for u, (kind, idx, cp) in enumerate(units):
-            if cp == 1:
-                ready[(kind, idx)] = u
-        burst_slots = [ready[("q", n)] + LAG_D for n in range(N_QK)]
 
         def grp_tile(u):
             if u not in grps:
-                grps[u] = grpp.tile([P, 2, BLK, 4], BF16, name="grp", tag="grp", align_bytes=64)
+                grps[u] = grpp.tile([P, GW, 4], BF16, name="grp", tag="grp", align_bytes=64)
             return grps[u]
 
-        def regroup(engine, u, lo, hi):
-            if lo < BLK < hi:
-                regroup(engine, u, lo, BLK)
-                regroup(engine, u, BLK, hi)
-            elif lo < hi:
-                regroup_piece(engine, u, lo // BLK, lo % BLK, hi - BLK * (lo // BLK))
-
-        def regroup_piece(engine, u, c2, lo, hi):
-            kind, idx, cp = units[u]
-            src = raw_piece(kind, idx, 2 * cp + c2)[:, :, lo:hi].rearrange("p t (c i) -> p c t i", i=RUN)
-            dst = grp_tile(u)[:, c2, lo:hi, :].rearrange("p (c i) t -> p c t i", i=RUN)
-            if engine == "V":
-                nc.vector.tensor_copy(out=dst, in_=src)
-            elif engine == "S":
-                nc.scalar.copy(out=dst, in_=src)
-            else:
-                src = raw_piece(kind, idx, 2 * cp + c2)[:, :, lo:hi].rearrange("p t w -> p w t")
-                dst = grp_tile(u)[:, c2, lo:hi, :]
-                nc.gpsimd.tensor_scalar(out=dst, in0=src, scalar1=live["gate"][:, 0:1], scalar2=0.0, op0=ALU.mult, op1=ALU.add)
-
-        def regroup_s(u):
-            regroup("S", u, 0, scalar_columns(u, n_units))
+        def s_columns(u):
+            if u < len(S_HEAD):
+                return S_HEAD[u]
+            if units[u][0] == "q":
+                return S_PAIR
+            return S_V if u < FIRST_PAIR + N_PAIR else S_TAIL
 
         def pool_columns(u):
-            if u < n_units and u - POOL_AHEAD in burst_slots[POOL_FIRST:]:
+            if u < n_units and units[u][0] == "q" and FIRST_PAIR <= u - POOL_AHEAD < FIRST_PAIR + N_PAIR:
                 return POOL_COLS
             return 0
+
+        def regroup(engine, u, lo, hi):
+            if lo >= hi:
+                return
+            if units[u][0] == "q":
+                src = loaded[units[u]][:, :, lo:hi]
+            elif lo < BLK < hi:
+                regroup(engine, u, lo, BLK)
+                regroup(engine, u, BLK, hi)
+                return
+            else:
+                half = lo // BLK
+                src = raw_piece(u, half)[:, :, lo - BLK * half:hi - BLK * half]
+            dst = grp_tile(u)[:, lo:hi, :]
+            if engine == "G":
+                nc.gpsimd.tensor_scalar(out=dst, in0=src.rearrange("p t w -> p w t"), scalar1=live["gate"][:, 0:1], scalar2=0.0, op0=ALU.mult, op1=ALU.add)
+                return
+            src = src.rearrange("p t (c i) -> p c t i", i=RUN)
+            dst = dst.rearrange("p (c i) t -> p c t i", i=RUN)
+            if engine == "V":
+                nc.vector.tensor_copy(out=dst, in_=src)
+            else:
+                nc.scalar.copy(out=dst, in_=src)
+
+        def regroup_s(u):
+            regroup("S", u, 0, s_columns(u))
+
+        def regroup_v(u):
+            regroup("V", u, s_columns(u), GW - pool_columns(u))
+            state["regrouped"] = u
 
         def regroup_g(u):
             if pool_columns(u) > 0:
                 live["gate"] = smal.tile([P, 1], F32, name="gate", tag="gate")
                 nc.vector.memset(live["gate"][:], 1.0)
-                regroup("G", u, 2 * BLK - pool_columns(u), 2 * BLK)
-
-        def regroup_v(u):
-            regroup("V", u, scalar_columns(u, n_units), 2 * BLK - pool_columns(u))
-            state["regrouped"] = u
+                regroup("G", u, GW - pool_columns(u), GW)
 
         def quantise(u):
-            cod = codp.tile([P, 2 * BLK], U32, name="cod", tag="cod", align_bytes=64)
-            scl = codp.tile([P, 2 * BLK], U8, name="scl", tag="scl", align_bytes=64)
-            nc.vector.quantize_mx(out=cod[:].bitcast(FP8X4), scales=scl[:], in_=grps[u][:].rearrange("p a w t -> p (a w t)"))
+            cod = codp.tile([P, GW], U32, name="cod", tag="cod", align_bytes=64)
+            scl = codp.tile([P, GW], U8, name="scl", tag="scl", align_bytes=64)
+            w = GW if u < n_units - 1 else BLK
+            for lo in range(0, GW, w):
+                nc.vector.quantize_mx(out=cod[:, lo:lo + w].bitcast(FP8X4), scales=scl[:, lo:lo + w], in_=grps[u][:, lo:lo + w, :].rearrange("p w t -> p (w t)"))
             cods[units[u]] = (cod, scl)
 
-        def store(s, b, h0, o_t):
-            nc.sync.dma_start(
-                out=outs[s][b, h0:h0 + 4, :, :].rearrange("h l d -> l h d"),
-                in_=o_t[:].rearrange("p (h d) -> p h d", h=4),
-            )
+        def project(i):
+            pt = psum.tile([P, 2, TOK], F32, name="pt", tag="pt", bufs=3)
+            live[("pt", i)] = pt
+            for hh in range(2):
+                lo = (2 * (i % 4) + hh) * HD
+                for c in range(PASSES):
+                    cod, scl = cods[("q", i // 4, c)]
+                    nc.tensor.matmul_mx(
+                        out=pt[:, hh, :],
+                        lhsT=cod[:, lo:lo + HD].bitcast(FP8X4),
+                        lhsT_scale=scl[:, lo:lo + HD],
+                        rhs=xqp[:, c, :, :, :].rearrange("p e b i -> p (e b i)").bitcast(FP8X4),
+                        rhs_scale=xsp[:, c, :, :, :].rearrange("p e b i -> p (e b i)"),
+                        start=(c == 0),
+                        stop=(c == PASSES - 1),
+                    )
 
-        def project(n):
-            for k in range(2):
-                pt = psum.tile([P, 2, TOK], F32, name="pt", tag="pt", bufs=PT_BUFS)
-                live[("pt", n, k)] = pt
-                for hh in range(2):
-                    j = 2 * k + hh
-                    for c in range(PASSES):
-                        cod, scl = cods[("q", n, c // 2)]
-                        lo = (c % 2) * BLK + j * HD
-                        nc.tensor.matmul_mx(
-                            out=pt[:, hh, :],
-                            lhsT=cod[:, lo:lo + HD].bitcast(FP8X4),
-                            lhsT_scale=scl[:, lo:lo + HD],
-                            rhs=xq[:, TOK * c:TOK * (c + 1)].bitcast(FP8X4),
-                            rhs_scale=xs[:, TOK * c:TOK * (c + 1)],
-                            start=(c == 0),
-                            stop=(c == PASSES - 1),
-                        )
-
-        def tables_times(n):
-            for j in range(4):
-                g = 4 * n + j
-                do = dop.tile([P, 2, TOK], F32, name="do", tag="do")
+        def tables_times(i):
+            do = dop.tile([P, 2, 2, B, 2, 64], F32, name="do", tag="do")
+            live[("do", i)] = do
+            for hh in range(2):
+                g = 2 * i + hh
                 nc.vector.scalar_tensor_tensor(
-                    out=do[:],
-                    in0=live[("pt", n, j // 2)][:, j % 2, :].unsqueeze(1).to_broadcast([P, 2, TOK]),
+                    out=do[:, :, :, :, hh, :],
+                    in0=live[("pt", i)][:, hh, :].rearrange("p (e b i) -> p e b i", e=2, b=B).unsqueeze(1).to_broadcast([P, 2, 2, B, 64]),
                     scalar=per_f[:, g:g + 1],
-                    in1=tabs[g // 16][:].rearrange("p d b l -> p d (b l)"),
+                    in1=tabs[g // 16][:],
                     op0=ALU.add,
                     op1=ALU.mult,
                 )
-                live[("do", g)] = do
 
-        def squares(n):
-            for j in range(4):
-                g = 4 * n + j
-                sq = dop.tile([P, TOK], F32, name="sq", tag="sq")
-                nc.scalar.activation(out=sq[:], in_=live[("pt", n, j // 2)][:, j % 2, :], func=ACT.Square, bias=per_f[:, g:g + 1], scale=1.0)
-                live[("sq", g)] = sq
+        def squares(i):
+            sq = dop.tile([P, 2, B, 2, 64], F32, name="sq", tag="sq")
+            live[("sq", i)] = sq
+            for hh in range(2):
+                g = 2 * i + hh
+                nc.scalar.activation(out=sq[:, :, :, hh, :], in_=live[("pt", i)][:, hh, :].rearrange("p (e b i) -> p e b i", e=2, b=B), func=ACT.Square, bias=per_f[:, g:g + 1], scale=1.0)
 
-        def turn(n):
-            ssb = psum.tile([P, 8, SS_N], F32, name="ssb", tag="ss", bufs=1)
-            live[("ss", n)] = ssb
-            for k in range(2):
-                rb = psum.tile([P, 2, B, P], F32, name="rb", tag="rb", bufs=2)
-                live[("rb", n, k)] = rb
-                for hh in range(2):
-                    j = 2 * k + hh
-                    g = 4 * n + j
-                    for b in range(B):
-                        nc.tensor.matmul(out=ssb[:, 2 * j + b, :], lhsT=live[("sq", g)][:, P * b:P * (b + 1)], rhs=ones[:], start=True, stop=True)
-                    for b in range(B):
-                        tok = slice(P * b, P * (b + 1))
-                        nc.tensor.matmul(out=rb[:, hh, b, :], lhsT=live[("do", g)][:, 0, tok], rhs=ident[:], is_transpose=True, start=True, stop=False)
-                        nc.tensor.matmul(out=rb[:, hh, b, :], lhsT=live[("do", g)][:, 1, tok], rhs=swp[:].rearrange("p i c -> p (i c)"), is_transpose=True, start=False, stop=True)
-
-        def norm_out(n):
-            rr = smal.tile([P, 8], F32, name="rr", tag="rr")
-            nc.scalar.activation(out=rr[:], in_=live[("ss", n)][:, :, 0], func=ACT.Abs_reciprocal_sqrt, bias=eps[:], scale=1.0 / HD)
-            o_ts = []
-            for b in range(B):
-                o_t = outp.tile([P, BLK], F32, name="o_t", tag="o_t")
-                o_ts.append(o_t)
-            for j in range(4):
+        def turn(i):
+            ssb = psum.tile([P, 2, B, SS_N], F32, name="ssb", tag="ss", bufs=1)
+            rb = psum.tile([P, 2, B, P], F32, name="rb", tag="rb", bufs=2)
+            live[("ss", i)] = ssb
+            live[("rb", i)] = rb
+            sq = live[("sq", i)]
+            do = live[("do", i)]
+            for e in range(2):
                 for b in range(B):
-                    nc.scalar.activation(out=o_ts[b][:, j * HD:(j + 1) * HD], in_=live[("rb", n, j // 2)][:, j % 2, b, :], func=ACT.Copy, scale=rr[:, 2 * j + b:2 * j + b + 1])
-            for b in range(B):
-                store(n // 4, b, (n % 4) * 4, o_ts[b])
+                    nc.tensor.matmul(out=ssb[:, e, b, :], lhsT=sq[:, e, b, :, :].rearrange("p h i -> p (h i)"), rhs=ones[:], start=True, stop=True)
+                for b in range(B):
+                    nc.tensor.matmul(out=rb[:, e, b, :], lhsT=do[:, 0, e, b, :, :].rearrange("p h i -> p (h i)"), rhs=ident[:], is_transpose=True, start=True, stop=False)
+                    nc.tensor.matmul(out=rb[:, e, b, :], lhsT=do[:, 1, e, b, :, :].rearrange("p h i -> p (h i)"), rhs=swp[:].rearrange("p i c -> p (i c)"), is_transpose=True, start=False, stop=True)
+
+        def norm_out(i):
+            rr = smal.tile([P, 2, B], F32, name="rr", tag="rr")
+            nc.scalar.activation(out=rr[:], in_=live[("ss", i)][:, :, :, 0], func=ACT.Abs_reciprocal_sqrt, bias=eps[:], scale=1.0 / HD)
+            o_t = outp.tile([P, B, 2, HD], F32, name="o_t", tag="o_t")
+            for e in range(2):
+                for b in range(B):
+                    nc.scalar.activation(out=o_t[:, b, e, :], in_=live[("rb", i)][:, e, b, :], func=ACT.Copy, scale=rr[:, e, b:b + 1])
+            h0 = (2 * i) % 16
+            nc.sync.dma_start(
+                out=outs[i // 8][:, h0:h0 + 2, :, :].rearrange("b h (i e) d -> (h i) b (e d)", e=2),
+                in_=o_t[:].rearrange("p b e d -> p b (e d)"),
+            )
 
         def multiply(u):
             kind, j, cp = units[u]
@@ -379,9 +357,12 @@ def tile_selfattention_pa_kernel(tc, x, pe, qkv_w, qkv_b, q_scale, k_scale, out_
 
         def add_bias(j):
             for b in range(B):
-                o_t = outp.tile([P, BLK], F32, name="o_t", tag="o_t")
+                o_t = outp.tile([P, BLK], F32, name="ov", tag="ov", bufs=4)
                 nc.vector.tensor_tensor(out=o_t[:], in0=live[("acc", j, b)][:], in1=bias_v[:, BLK * j:BLK * (j + 1)], op=ALU.add)
-                store(2, b, 4 * j, o_t)
+                nc.sync.dma_start(
+                    out=outs[2][b, 4 * j:4 * j + 4, :, :].rearrange("h l d -> l h d"),
+                    in_=o_t[:].rearrange("p (h d) -> p h d", h=4),
+                )
 
         for u in range(AHEAD_S):
             regroup_s(u)
@@ -391,34 +372,35 @@ def tile_selfattention_pa_kernel(tc, x, pe, qkv_w, qkv_b, q_scale, k_scale, out_
         tables()
         for cp in range(2):
             x_turn(cp)
-        v_bias()
-        for k in range(n_units + LAG_O + 1):
+        for k in range(n_units + 2):
+            i = k - FIRST_PAIR
+            if 0 < i < N_PAIR:
+                squares(i)
             if k + AHEAD_S < n_units:
                 regroup_s(k + AHEAD_S)
+            if i == 0:
+                squares(i)
+            if 0 <= i - LAG_O < N_PAIR:
+                norm_out(i - LAG_O)
+            if k == VB_STEP:
+                v_bias()
             if k + AHEAD_V < n_units:
                 regroup_v(k + AHEAD_V)
             loads()
             if k < n_units:
                 quantise(k)
-            if k == 0:
-                for cp in range(2):
+            for cp in range(2):
+                if k == X_STEP[cp]:
                     x_quantise(cp)
-            for n in range(N_QK):
-                if ready[("q", n)] + LAG_O == k:
-                    norm_out(n)
-            for j in range(N_V):
-                if ready[("v", j)] + 1 == k:
-                    add_bias(j)
-            for n in range(N_QK):
-                if ready[("q", n)] == k:
-                    project(n)
+            if k == X_STEP[1]:
+                x_by_parity()
+            if k >= 1 and k - 1 < n_units and units[k - 1][0] == "v" and units[k - 1][2] == 1:
+                add_bias(units[k - 1][1])
+            if 0 <= i + 1 < N_PAIR:
+                project(i + 1)
             if k < n_units and units[k][0] == "v":
                 multiply(k)
-            for n in range(N_QK):
-                if ready[("q", n)] + LAG_D == k:
-                    regroup_g(k + POOL_AHEAD)
-                    tables_times(n)
-            for n in range(N_QK):
-                if ready[("q", n)] + LAG_SQ == k:
-                    squares(n)
-                    turn(n)
+            if 0 <= i < N_PAIR:
+                regroup_g(k + POOL_AHEAD)
+                tables_times(i)
+                turn(i)

@@ -40,7 +40,9 @@ RUN = 8
 POOL_COLS = 192
 POOL_AHEAD = 2
 S_HEAD = (512, 448, 448, 448)
-S_PAIR = 448
+S_PAIR = 512
+PE_COLS = 256
+PE_UNITS = range(4, 16)
 S_V = 512
 S_TAIL = 608
 X_STEP = (1, 2)
@@ -125,6 +127,8 @@ def tile_selfattention_pa_kernel(tc, x, pe, qkv_w, qkv_b, q_scale, k_scale, out_
         nc.gpsimd.tensor_copy(out=swp[:, :, 1], in_=idv[:, :, 0])
         eps = const.tile([P, 1], F32, name="eps")
         nc.vector.memset(eps[:], EPS)
+        warm = const.tile([P, 1], F32, name="warm")
+        nc.scalar.activation(out=warm[:], in_=eps[:], func=ACT.Abs_reciprocal_sqrt, bias=eps[:], scale=1.0)
         ones = const.tile([P, SS_N], F32, name="ones")
         nc.vector.memset(ones[:], 1.0)
         hrows = const.tile([P, P], BF16, name="hrows")
@@ -251,7 +255,28 @@ def tile_selfattention_pa_kernel(tc, x, pe, qkv_w, qkv_b, q_scale, k_scale, out_
                 nc.scalar.copy(out=dst, in_=src)
 
         def regroup_s(u):
-            regroup("S", u, 0, s_columns(u))
+            if u not in PE_UNITS:
+                regroup("S", u, 0, s_columns(u))
+                return
+            lo = s_columns(u) - PE_COLS
+            regroup("S", u, 0, lo)
+            nc.scalar.copy(out=grp_tile(u)[:, lo:lo + PE_COLS, :], in_=live[("bank", u)][:])
+
+        def regroup_t(u):
+            if u not in PE_UNITS:
+                return
+            lo = s_columns(u) - PE_COLS
+            bank = psum.tile([P, PE_COLS, 4], BF16, name="gbank", tag="va", bufs=2)
+            live[("bank", u)] = bank
+            for h in range(2):
+                w0 = lo + P * h
+                nc.tensor.matmul(
+                    out=bank[:, P * h:P * (h + 1), :].rearrange("p w t -> p (w t)"),
+                    lhsT=identb[:],
+                    rhs=loaded[units[u]][:, :, w0:w0 + P].rearrange("p t w -> p w t"),
+                    start=True,
+                    stop=True,
+                )
 
         def regroup_v(u):
             regroup("V", u, s_columns(u), GW - pool_columns(u))
@@ -400,6 +425,7 @@ def tile_selfattention_pa_kernel(tc, x, pe, qkv_w, qkv_b, q_scale, k_scale, out_
                 project(i + 1)
             if k < n_units and units[k][0] == "v":
                 multiply(k)
+            regroup_t(k + AHEAD_S + 1)
             if 0 <= i < N_PAIR:
                 regroup_g(k + POOL_AHEAD)
                 tables_times(i)

@@ -26,7 +26,7 @@ FLOPS = 2 * 256 * 2048 * 6144
 N_QK = 4
 N_V = 2
 N_PAIR = 16
-SS_N = 64
+SS_N = 32
 RAW_BUFS = 9
 GRP_BUFS = 4
 COD_BUFS = 9
@@ -34,7 +34,8 @@ DO_BUFS = 3
 OUT_BUFS = 5
 AHEAD_S = 2
 AHEAD_V = 1
-FIRST_PAIR = 4
+FIRST_PAIR = 5
+AHEAD_P = 2
 LAG_O = 1
 RUN = 8
 POOL_COLS = 192
@@ -43,8 +44,8 @@ S_HEAD = (512, 448, 448, 448)
 S_PAIR = 512
 PE_COLS = 256
 PE_UNITS = range(4, 16)
-S_V = 512
-S_TAIL = 608
+S_V = 416
+S_TAIL = 560
 X_STEP = (1, 2)
 VB_STEP = 2
 
@@ -227,7 +228,7 @@ def tile_selfattention_pa_kernel(tc, x, pe, qkv_w, qkv_b, q_scale, k_scale, out_
             return S_V if u < FIRST_PAIR + N_PAIR else S_TAIL
 
         def pool_columns(u):
-            if u < n_units and units[u][0] == "q" and FIRST_PAIR <= u - POOL_AHEAD < FIRST_PAIR + N_PAIR:
+            if u < n_units and FIRST_PAIR <= u - POOL_AHEAD < FIRST_PAIR + N_PAIR:
                 return POOL_COLS
             return 0
 
@@ -334,16 +335,18 @@ def tile_selfattention_pa_kernel(tc, x, pe, qkv_w, qkv_b, q_scale, k_scale, out_
                 g = 2 * i + hh
                 nc.scalar.activation(out=sq[:, :, :, hh, :], in_=live[("pt", i)][:, hh, :].rearrange("p (e b i) -> p e b i", e=2, b=B), func=ACT.Square, bias=per_f[:, g:g + 1], scale=1.0)
 
-        def turn(i):
+        def sum_squares(i):
             ssb = psum.tile([P, 2, B, SS_N], F32, name="ssb", tag="ss", bufs=1)
-            rb = psum.tile([P, 2, B, P], F32, name="rb", tag="rb", bufs=2)
             live[("ss", i)] = ssb
-            live[("rb", i)] = rb
-            sq = live[("sq", i)]
-            do = live[("do", i)]
             for e in range(2):
                 for b in range(B):
-                    nc.tensor.matmul(out=ssb[:, e, b, :], lhsT=sq[:, e, b, :, :].rearrange("p h i -> p (h i)"), rhs=ones[:], start=True, stop=True)
+                    nc.tensor.matmul(out=ssb[:, e, b, :], lhsT=live[("sq", i)][:, e, b, :, :].rearrange("p h i -> p (h i)"), rhs=ones[:], start=True, stop=True)
+
+        def turn(i):
+            rb = psum.tile([P, 2, B, P], F32, name="rb", tag="rb", bufs=2)
+            live[("rb", i)] = rb
+            do = live[("do", i)]
+            for e in range(2):
                 for b in range(B):
                     nc.tensor.matmul(out=rb[:, e, b, :], lhsT=do[:, 0, e, b, :, :].rearrange("p h i -> p (h i)"), rhs=ident[:], is_transpose=True, start=True, stop=False)
                     nc.tensor.matmul(out=rb[:, e, b, :], lhsT=do[:, 1, e, b, :, :].rearrange("p h i -> p (h i)"), rhs=swp[:].rearrange("p i c -> p (i c)"), is_transpose=True, start=False, stop=True)
@@ -421,12 +424,13 @@ def tile_selfattention_pa_kernel(tc, x, pe, qkv_w, qkv_b, q_scale, k_scale, out_
                 x_by_parity()
             if k >= 1 and k - 1 < n_units and units[k - 1][0] == "v" and units[k - 1][2] == 1:
                 add_bias(units[k - 1][1])
-            if 0 <= i + 1 < N_PAIR:
-                project(i + 1)
+            if 0 <= i + AHEAD_P < N_PAIR:
+                project(i + AHEAD_P)
             if k < n_units and units[k][0] == "v":
                 multiply(k)
             regroup_t(k + AHEAD_S + 1)
             if 0 <= i < N_PAIR:
+                sum_squares(i)
                 regroup_g(k + POOL_AHEAD)
                 tables_times(i)
                 turn(i)

@@ -26,7 +26,7 @@ FLOPS = 2 * 256 * 2048 * 6144
 N_QK = 4
 N_V = 2
 N_PAIR = 16
-SS_N = 32
+SS_N = 64
 RAW_BUFS = 9
 GRP_BUFS = 4
 COD_BUFS = 9
@@ -335,18 +335,16 @@ def tile_selfattention_pa_kernel(tc, x, pe, qkv_w, qkv_b, q_scale, k_scale, out_
                 g = 2 * i + hh
                 nc.scalar.activation(out=sq[:, :, :, hh, :], in_=live[("pt", i)][:, hh, :].rearrange("p (e b i) -> p e b i", e=2, b=B), func=ACT.Square, bias=per_f[:, g:g + 1], scale=1.0)
 
-        def sum_squares(i):
+        def turn(i):
             ssb = psum.tile([P, 2, B, SS_N], F32, name="ssb", tag="ss", bufs=1)
             live[("ss", i)] = ssb
-            for e in range(2):
-                for b in range(B):
-                    nc.tensor.matmul(out=ssb[:, e, b, :], lhsT=live[("sq", i)][:, e, b, :, :].rearrange("p h i -> p (h i)"), rhs=ones[:], start=True, stop=True)
-
-        def turn(i):
+            sq = live[("sq", i)]
             rb = psum.tile([P, 2, B, P], F32, name="rb", tag="rb", bufs=2)
             live[("rb", i)] = rb
             do = live[("do", i)]
             for e in range(2):
+                for b in range(B):
+                    nc.tensor.matmul(out=ssb[:, e, b, :], lhsT=sq[:, e, b, :, :].rearrange("p h i -> p (h i)"), rhs=ones[:], start=True, stop=True)
                 for b in range(B):
                     nc.tensor.matmul(out=rb[:, e, b, :], lhsT=do[:, 0, e, b, :, :].rearrange("p h i -> p (h i)"), rhs=ident[:], is_transpose=True, start=True, stop=False)
                     nc.tensor.matmul(out=rb[:, e, b, :], lhsT=do[:, 1, e, b, :, :].rearrange("p h i -> p (h i)"), rhs=swp[:].rearrange("p i c -> p (i c)"), is_transpose=True, start=False, stop=True)
@@ -430,7 +428,6 @@ def tile_selfattention_pa_kernel(tc, x, pe, qkv_w, qkv_b, q_scale, k_scale, out_
                 multiply(k)
             regroup_t(k + AHEAD_S + 1)
             if 0 <= i < N_PAIR:
-                sum_squares(i)
                 regroup_g(k + POOL_AHEAD)
                 tables_times(i)
                 turn(i)

@@ -38,14 +38,14 @@ FIRST_PAIR = 5
 AHEAD_P = 2
 LAG_O = 1
 RUN = 8
-POOL_COLS = 192
+POOL_COLS = 160
 POOL_AHEAD = 2
 S_HEAD = (512, 448, 448, 448)
-S_PAIR = 512
+S_PAIR = 576
 PE_COLS = 256
 PE_UNITS = range(4, 16)
-S_V = 416
-S_TAIL = 560
+S_V = 512
+S_TAIL = 640
 X_STEP = (1, 2)
 VB_STEP = 2
 

@@ -27,11 +27,11 @@ N_QK = 4
 N_V = 2
 N_PAIR = 16
 SS_N = 64
-RAW_BUFS = 9
+RAW_BUFS = 7
 GRP_BUFS = 4
 COD_BUFS = 9
 DO_BUFS = 3
-OUT_BUFS = 5
+OUT_BUFS = 8
 AHEAD_S = 2
 AHEAD_V = 1
 FIRST_PAIR = 5

@@ -41,11 +41,11 @@ RUN = 8
 POOL_COLS = 160
 POOL_AHEAD = 2
 S_HEAD = (512, 448, 448, 448)
-S_PAIR = 576
+S_PAIR = 544
 PE_COLS = 256
 PE_UNITS = range(4, 16)
-S_V = 512
-S_TAIL = 640
+S_V = 480
+S_TAIL = 608
 X_STEP = (1, 2)
 VB_STEP = 2
 
@@ -365,21 +365,21 @@ def tile_selfattention_pa_kernel(tc, x, pe, qkv_w, qkv_b, q_scale, k_scale, out_
         def multiply(u):
             kind, j, cp = units[u]
             cod, scl = cods[units[u]]
-            for c2 in range(2):
+            passes = [(c2, b) for b in range(B) for c2 in range(2)]
+            for c2, b in passes if u < n_units - 1 else sorted(passes):
                 c = 2 * cp + c2
-                for b in range(B):
-                    if c == 0:
-                        live[("acc", j, b)] = psum.tile([P, BLK], F32, name="acc", tag="va", bufs=2)
-                    lo = (c * B + b) * P
-                    nc.tensor.matmul_mx(
-                        out=live[("acc", j, b)][:],
-                        lhsT=xq[:, lo:lo + P].bitcast(FP8X4),
-                        lhsT_scale=xs[:, lo:lo + P],
-                        rhs=cod[:, c2 * BLK:(c2 + 1) * BLK].bitcast(FP8X4),
-                        rhs_scale=scl[:, c2 * BLK:(c2 + 1) * BLK],
-                        start=(c == 0),
-                        stop=(c == PASSES - 1),
-                    )
+                if c == 0:
+                    live[("acc", j, b)] = psum.tile([P, BLK], F32, name="acc", tag="va", bufs=2)
+                lo = (c * B + b) * P
+                nc.tensor.matmul_mx(
+                    out=live[("acc", j, b)][:],
+                    lhsT=xq[:, lo:lo + P].bitcast(FP8X4),
+                    lhsT_scale=xs[:, lo:lo + P],
+                    rhs=cod[:, c2 * BLK:(c2 + 1) * BLK].bitcast(FP8X4),
+                    rhs_scale=scl[:, c2 * BLK:(c2 + 1) * BLK],
+                    start=(c == 0),
+                    stop=(c == PASSES - 1),
+                )
 
         def add_bias(j):
             for b in range(B):
@@ -400,12 +400,10 @@ def tile_selfattention_pa_kernel(tc, x, pe, qkv_w, qkv_b, q_scale, k_scale, out_
             x_turn(cp)
         for k in range(n_units + 2):
             i = k - FIRST_PAIR
-            if 0 < i < N_PAIR:
+            if 0 <= i < N_PAIR:
                 squares(i)
             if k + AHEAD_S < n_units:
                 regroup_s(k + AHEAD_S)
-            if i == 0:
-                squares(i)
             if 0 <= i - LAG_O < N_PAIR:
                 norm_out(i - LAG_O)
             if k == VB_STEP:

from contextlib import ExitStack

import concourse.mybir as mybir
from concourse.masks import make_identity

F32 = mybir.dt.float32
BF16 = mybir.dt.bfloat16
U32 = mybir.dt.uint32
U8 = mybir.dt.uint8
I32 = mybir.dt.int32
FP8X4 = mybir.dt.float8_e4m3fn_x4
ALU = mybir.AluOpType
ACT = mybir.ActivationFunctionType

P = 128
B = 2
DIM = 2048
HD = 128
PASSES = 4
BLK = 512
GW = 1024
TOK = B * P
EPS = 1e-6
FLOPS = 2 * 256 * 2048 * 6144

N_QK = 4
N_V = 2
N_PAIR = 16
SS_N = 64
RAW_BUFS = 7
GRP_BUFS = 4
COD_BUFS = 9
DO_BUFS = 3
OUT_BUFS = 8
AHEAD_S = 2
AHEAD_V = 1
FIRST_PAIR = 5
AHEAD_P = 2
LAG_O = 1
RUN = 8
POOL_COLS = 160
POOL_AHEAD = 2
S_HEAD = (512, 448, 448, 448)
S_PAIR = 544
PE_COLS = 256
PE_UNITS = range(4, 16)
S_V = 480
S_TAIL = 608
X_STEP = (1, 2)
VB_STEP = 2


def unit_list():
    units = []
    for n in range(N_QK):
        for c in range(PASSES):
            units.append(("q", n, c))
    for j in range(2 * N_V):
        for cp in range(2):
            units.append(("v", j, cp))
    return units


def tile_selfattention_pa_kernel(tc, x, pe, qkv_w, qkv_b, q_scale, k_scale, out_0, out_1, out_2):
    nc = tc.nc
    outs = (out_0, out_1, out_2)
    units = unit_list()
    n_units = len(units)
    with ExitStack() as ctx:
        ctx.enter_context(tc.manual_schedule())
        const = ctx.enter_context(tc.tile_pool(name="const", bufs=1))
        rawp = ctx.enter_context(tc.tile_pool(name="rawp", bufs=1))
        grpp = ctx.enter_context(tc.tile_pool(name="grpp", bufs=GRP_BUFS))
        codp = ctx.enter_context(tc.tile_pool(name="codp", bufs=COD_BUFS))
        dop = ctx.enter_context(tc.tile_pool(name="dop", bufs=DO_BUFS))
        outp = ctx.enter_context(tc.tile_pool(name="outp", bufs=OUT_BUFS))
        smal = ctx.enter_context(tc.tile_pool(name="smal", bufs=3))
        psum = ctx.enter_context(tc.psum_pool(name="psum", bufs=1))

        load_order = []
        last_reader = {}
        for u, (kind, idx, c) in enumerate(units):
            if kind == "q":
                keys = [("q", idx, c)]
            else:
                keys = [("v", idx // 2, 2 * c), ("v", idx // 2, 2 * c + 1)]
            for key in keys:
                if key not in last_reader:
                    load_order.append(key)
                last_reader[key] = u
        loaded = {}
        state = {"next_load": 0, "regrouped": -1}

        def issue_load(key, pieces):
            kind, idx, c = key
            lo = GW * idx if kind == "q" else GW * (N_QK + idx)
            rw = rawp.tile([P, 4, GW], BF16, name="raw", tag="raw", bufs=RAW_BUFS)
            w = GW // pieces
            for i in range(pieces):
                src = qkv_w[512 * c:512 * (c + 1), lo + w * i:lo + w * (i + 1)]
                nc.sync.dma_start(out=rw[:, :, w * i:w * (i + 1)], in_=src.rearrange("(p j) w -> p j w", j=4))
            loaded[key] = rw

        def loads(limit=None, pieces=1):
            n = 0
            while state["next_load"] < len(load_order) and (limit is None or n < limit):
                i = state["next_load"]
                if i >= RAW_BUFS and last_reader[load_order[i - RAW_BUFS]] > state["regrouped"]:
                    break
                issue_load(load_order[i], pieces)
                state["next_load"] += 1
                n += 1

        def raw_piece(u, half):
            kind, idx, c = units[u]
            if kind == "q":
                return loaded[units[u]][:, :, BLK * half:BLK * (half + 1)]
            j = idx % 2
            return loaded[("v", idx // 2, 2 * c + half)][:, :, BLK * j:BLK * (j + 1)]

        ident = const.tile([P, P], F32, name="ident")
        make_identity(nc, ident[:])
        identb = const.tile([P, P], BF16, name="identb")
        make_identity(nc, identb[:])
        swp = const.tile([P, 64, 2], F32, name="swp")
        idv = ident[:].rearrange("p (i c) -> p i c", c=2)
        nc.gpsimd.tensor_copy(out=swp[:, :, 0], in_=idv[:, :, 1])
        nc.gpsimd.tensor_copy(out=swp[:, :, 1], in_=idv[:, :, 0])
        eps = const.tile([P, 1], F32, name="eps")
        nc.vector.memset(eps[:], EPS)
        warm = const.tile([P, 1], F32, name="warm")
        nc.scalar.activation(out=warm[:], in_=eps[:], func=ACT.Abs_reciprocal_sqrt, bias=eps[:], scale=1.0)
        ones = const.tile([P, SS_N], F32, name="ones")
        nc.vector.memset(ones[:], 1.0)
        hrows = const.tile([P, P], BF16, name="hrows")
        nc.vector.memset(hrows[:].bitcast(I32), 0)
        vrows = const.tile([P, BLK], BF16, name="vrows")
        nc.vector.memset(vrows[:].bitcast(I32), 0)

        loads(1, 2)
        nc.sync.dma_start(out=hrows[0:32, :], in_=qkv_b[0:4096].rearrange("(j n) -> j n", n=HD))
        nc.sync.dma_start(out=hrows[32:33, :], in_=q_scale.rearrange("(o n) -> o n", o=1))
        nc.sync.dma_start(out=hrows[33:34, :], in_=k_scale.rearrange("(o n) -> o n", o=1))
        pe_sb = const.tile([P, 256], BF16, name="pe_sb")
        nc.sync.dma_start(out=pe_sb[:], in_=pe.rearrange("a b l i r c -> (a b l) (i r c)"))
        loads(1)
        x_sb = const.tile([P, B, DIM], BF16, name="x_sb")
        for b in range(B):
            nc.sync.dma_start(out=x_sb[:, b, :], in_=x[b])
        nc.sync.dma_start(out=vrows[0:4, :], in_=qkv_b[4096:6144].rearrange("(j n) -> j n", n=BLK))
        loads()

        per_f = const.tile([P, 34], F32, name="per_f")
        pel = const.tile([P, 2, 64, 2], F32, name="pel")
        tabs = []
        bias_v = const.tile([P, 2 * N_V * BLK], BF16, name="bias_v")

        def per_feature():
            hps = psum.tile([P, P], BF16, name="hps", tag="rb", bufs=2)
            nc.tensor.transpose(hps[:], hrows[:], identb[:])
            nc.vector.tensor_copy(out=per_f[:], in_=hps[:, 0:34])
            pev = pe_sb[:].rearrange("p (i x) -> p i x", x=4)
            nc.vector.tensor_copy(out=pel[:, 0, :, :], in_=pev[:, :, 0:4:3])
            nc.vector.tensor_copy(out=pel[:, 1, :, 0], in_=pev[:, :, 2])
            nc.vector.tensor_copy(out=pel[:, 1, :, 1], in_=pev[:, :, 1])

        def tables():
            tps = psum.tile([P, 2, P], F32, name="tps", tag="rb", bufs=2)
            for d in range(2):
                nc.tensor.transpose(tps[:, d, :], pel[:, d, :, :].rearrange("p i c -> p (i c)"), ident[:])
            for s in range(2):
                tab = const.tile([P, 2, 2, B, 64], F32, name="tab%d" % s)
                for b in range(B):
                    nc.scalar.activation(out=tab[:, :, :, b, :], in_=tps[:].rearrange("p d (i e) -> p d e i", e=2), func=ACT.Copy, scale=per_f[:, 32 + s:33 + s])
                tabs.append(tab)

        def v_bias():
            for i in range(2):
                bank = psum.tile([P, 2, BLK], BF16, name="bank", tag="va", bufs=2)
                for h in range(2):
                    j = 2 * i + h
                    nc.tensor.matmul(out=bank[:, h, :], lhsT=identb[:, j:j + 1].to_broadcast([P, P]), rhs=vrows[:], start=True, stop=True)
                nc.scalar.copy(out=bias_v[:, 2 * BLK * i:2 * BLK * (i + 1)], in_=bank[:].rearrange("p h n -> p (h n)"))

        xw = x_sb[:].bitcast(F32)
        xg = const.tile([P, 4 * B * P * PASSES], BF16, name="xg", align_bytes=64)
        xgw = xg[:].bitcast(F32).rearrange("p (c b r u) -> p c b r u", c=PASSES, b=B, r=P, u=2)
        xq = const.tile([P, PASSES * B * P], U32, name="xq", align_bytes=64)
        xs = const.tile([P, PASSES * B * P], U8, name="xs", align_bytes=64)

        xqp = const.tile([P, PASSES, 2, B, 64], U32, name="xqp", align_bytes=64)
        xsp = const.tile([P, PASSES, 2, B, 64], U8, name="xsp", align_bytes=64)

        def x_by_parity():
            nc.vector.tensor_copy(out=xqp[:], in_=xq[:].rearrange("p (c b i e) -> p c e b i", c=PASSES, b=B, e=2))
            nc.vector.tensor_copy(out=xsp[:], in_=xs[:].rearrange("p (c b i e) -> p c e b i", c=PASSES, b=B, e=2))

        def x_turn(cp):
            for b in range(B):
                xt = psum.tile([P, 2, 2, P], F32, name="xt", tag="va" if b == 0 else "pt", bufs=2 if b == 0 else 3)
                for c2 in range(2):
                    c = 2 * cp + c2
                    for u in range(2):
                        nc.tensor.transpose(xt[:, c2, u, :], xw[:, b, 256 * c + u:256 * (c + 1):2], ident[:])
                nc.scalar.copy(out=xgw[:, 2 * cp:2 * cp + 2, b, :, :], in_=xt[:].rearrange("p c u r -> p c r u"))

        def x_quantise(cp):
            nc.vector.quantize_mx(
                out=xq[:, 512 * cp:512 * (cp + 1)].bitcast(FP8X4),
                scales=xs[:, 512 * cp:512 * (cp + 1)],
                in_=xg[:, 2048 * cp:2048 * (cp + 1)],
            )

        grps = {}
        cods = {}
        live = {}

        def grp_tile(u):
            if u not in grps:
                grps[u] = grpp.tile([P, GW, 4], BF16, name="grp", tag="grp", align_bytes=64)
            return grps[u]

        def s_columns(u):
            if u < len(S_HEAD):
                return S_HEAD[u]
            if units[u][0] == "q":
                return S_PAIR
            return S_V if u < FIRST_PAIR + N_PAIR else S_TAIL

        def pool_columns(u):
            if u < n_units and FIRST_PAIR <= u - POOL_AHEAD < FIRST_PAIR + N_PAIR:
                return POOL_COLS
            return 0

        def regroup(engine, u, lo, hi):
            if lo >= hi:
                return
            if units[u][0] == "q":
                src = loaded[units[u]][:, :, lo:hi]
            elif lo < BLK < hi:
                regroup(engine, u, lo, BLK)
                regroup(engine, u, BLK, hi)
                return
            else:
                half = lo // BLK
                src = raw_piece(u, half)[:, :, lo - BLK * half:hi - BLK * half]
            dst = grp_tile(u)[:, lo:hi, :]
            if engine == "G":
                nc.gpsimd.tensor_scalar(out=dst, in0=src.rearrange("p t w -> p w t"), scalar1=live["gate"][:, 0:1], scalar2=0.0, op0=ALU.mult, op1=ALU.add)
                return
            src = src.rearrange("p t (c i) -> p c t i", i=RUN)
            dst = dst.rearrange("p (c i) t -> p c t i", i=RUN)
            if engine == "V":
                nc.vector.tensor_copy(out=dst, in_=src)
            else:
                nc.scalar.copy(out=dst, in_=src)

        def regroup_s(u):
            if u not in PE_UNITS:
                regroup("S", u, 0, s_columns(u))
                return
            lo = s_columns(u) - PE_COLS
            regroup("S", u, 0, lo)
            nc.scalar.copy(out=grp_tile(u)[:, lo:lo + PE_COLS, :], in_=live[("bank", u)][:])

        def regroup_t(u):
            if u not in PE_UNITS:
                return
            lo = s_columns(u) - PE_COLS
            bank = psum.tile([P, PE_COLS, 4], BF16, name="gbank", tag="va", bufs=2)
            live[("bank", u)] = bank
            for h in range(2):
                w0 = lo + P * h
                nc.tensor.matmul(
                    out=bank[:, P * h:P * (h + 1), :].rearrange("p w t -> p (w t)"),
                    lhsT=identb[:],
                    rhs=loaded[units[u]][:, :, w0:w0 + P].rearrange("p t w -> p w t"),
                    start=True,
                    stop=True,
                )

        def regroup_v(u):
            regroup("V", u, s_columns(u), GW - pool_columns(u))
            state["regrouped"] = u

        def regroup_g(u):
            if pool_columns(u) > 0:
                live["gate"] = smal.tile([P, 1], F32, name="gate", tag="gate")
                nc.vector.memset(live["gate"][:], 1.0)
                regroup("G", u, GW - pool_columns(u), GW)

        def quantise(u):
            cod = codp.tile([P, GW], U32, name="cod", tag="cod", align_bytes=64)
            scl = codp.tile([P, GW], U8, name="scl", tag="scl", align_bytes=64)
            w = GW if u < n_units - 1 else BLK
            for lo in range(0, GW, w):
                nc.vector.quantize_mx(out=cod[:, lo:lo + w].bitcast(FP8X4), scales=scl[:, lo:lo + w], in_=grps[u][:, lo:lo + w, :].rearrange("p w t -> p (w t)"))
            cods[units[u]] = (cod, scl)

        def project(i):
            pt = psum.tile([P, 2, TOK], F32, name="pt", tag="pt", bufs=3)
            live[("pt", i)] = pt
            for hh in range(2):
                lo = (2 * (i % 4) + hh) * HD
                for c in range(PASSES):
                    cod, scl = cods[("q", i // 4, c)]
                    nc.tensor.matmul_mx(
                        out=pt[:, hh, :],
                        lhsT=cod[:, lo:lo + HD].bitcast(FP8X4),
                        lhsT_scale=scl[:, lo:lo + HD],
                        rhs=xqp[:, c, :, :, :].rearrange("p e b i -> p (e b i)").bitcast(FP8X4),
                        rhs_scale=xsp[:, c, :, :, :].rearrange("p e b i -> p (e b i)"),
                        start=(c == 0),
                        stop=(c == PASSES - 1),
                    )

        def tables_times(i):
            do = dop.tile([P, 2, 2, B, 2, 64], F32, name="do", tag="do")
            live[("do", i)] = do
            for hh in range(2):
                g = 2 * i + hh
                nc.vector.scalar_tensor_tensor(
                    out=do[:, :, :, :, hh, :],
                    in0=live[("pt", i)][:, hh, :].rearrange("p (e b i) -> p e b i", e=2, b=B).unsqueeze(1).to_broadcast([P, 2, 2, B, 64]),
                    scalar=per_f[:, g:g + 1],
                    in1=tabs[g // 16][:],
                    op0=ALU.add,
                    op1=ALU.mult,
                )

        def squares(i):
            sq = dop.tile([P, 2, B, 2, 64], F32, name="sq", tag="sq")
            live[("sq", i)] = sq
            for hh in range(2):
                g = 2 * i + hh
                nc.scalar.activation(out=sq[:, :, :, hh, :], in_=live[("pt", i)][:, hh, :].rearrange("p (e b i) -> p e b i", e=2, b=B), func=ACT.Square, bias=per_f[:, g:g + 1], scale=1.0)

        def turn(i):
            ssb = psum.tile([P, 2, B, SS_N], F32, name="ssb", tag="ss", bufs=1)
            live[("ss", i)] = ssb
            sq = live[("sq", i)]
            rb = psum.tile([P, 2, B, P], F32, name="rb", tag="rb", bufs=2)
            live[("rb", i)] = rb
            do = live[("do", i)]
            for e in range(2):
                for b in range(B):
                    nc.tensor.matmul(out=ssb[:, e, b, :], lhsT=sq[:, e, b, :, :].rearrange("p h i -> p (h i)"), rhs=ones[:], start=True, stop=True)
                for b in range(B):
                    nc.tensor.matmul(out=rb[:, e, b, :], lhsT=do[:, 0, e, b, :, :].rearrange("p h i -> p (h i)"), rhs=ident[:], is_transpose=True, start=True, stop=False)
                    nc.tensor.matmul(out=rb[:, e, b, :], lhsT=do[:, 1, e, b, :, :].rearrange("p h i -> p (h i)"), rhs=swp[:].rearrange("p i c -> p (i c)"), is_transpose=True, start=False, stop=True)

        def norm_out(i):
            rr = smal.tile([P, 2, B], F32, name="rr", tag="rr")
            nc.scalar.activation(out=rr[:], in_=live[("ss", i)][:, :, :, 0], func=ACT.Abs_reciprocal_sqrt, bias=eps[:], scale=1.0 / HD)
            o_t = outp.tile([P, B, 2, HD], F32, name="o_t", tag="o_t")
            for e in range(2):
                for b in range(B):
                    nc.scalar.activation(out=o_t[:, b, e, :], in_=live[("rb", i)][:, e, b, :], func=ACT.Copy, scale=rr[:, e, b:b + 1])
            h0 = (2 * i) % 16
            nc.sync.dma_start(
                out=outs[i // 8][:, h0:h0 + 2, :, :].rearrange("b h (i e) d -> (h i) b (e d)", e=2),
                in_=o_t[:].rearrange("p b e d -> p b (e d)"),
            )

        def multiply(u):
            kind, j, cp = units[u]
            cod, scl = cods[units[u]]
            passes = [(c2, b) for b in range(B) for c2 in range(2)]
            for c2, b in passes if u < n_units - 1 else sorted(passes):
                c = 2 * cp + c2
                if c == 0:
                    live[("acc", j, b)] = psum.tile([P, BLK], F32, name="acc", tag="va", bufs=2)
                lo = (c * B + b) * P
                nc.tensor.matmul_mx(
                    out=live[("acc", j, b)][:],
                    lhsT=xq[:, lo:lo + P].bitcast(FP8X4),
                    lhsT_scale=xs[:, lo:lo + P],
                    rhs=cod[:, c2 * BLK:(c2 + 1) * BLK].bitcast(FP8X4),
                    rhs_scale=scl[:, c2 * BLK:(c2 + 1) * BLK],
                    start=(c == 0),
                    stop=(c == PASSES - 1),
                )

        def add_bias(j):
            for b in range(B):
                o_t = outp.tile([P, BLK], F32, name="ov", tag="ov", bufs=4)
                nc.vector.tensor_tensor(out=o_t[:], in0=live[("acc", j, b)][:], in1=bias_v[:, BLK * j:BLK * (j + 1)], op=ALU.add)
                nc.sync.dma_start(
                    out=outs[2][b, 4 * j:4 * j + 4, :, :].rearrange("h l d -> l h d"),
                    in_=o_t[:].rearrange("p (h d) -> p h d", h=4),
                )

        for u in range(AHEAD_S):
            regroup_s(u)
            if u < AHEAD_V:
                regroup_v(u)
        per_feature()
        tables()
        for cp in range(2):
            x_turn(cp)
        for k in range(n_units + 2):
            i = k - FIRST_PAIR
            if 0 <= i < N_PAIR:
                squares(i)
            if k + AHEAD_S < n_units:
                regroup_s(k + AHEAD_S)
            if 0 <= i - LAG_O < N_PAIR:
                norm_out(i - LAG_O)
            if k == VB_STEP:
                v_bias()
            if k + AHEAD_V < n_units:
                regroup_v(k + AHEAD_V)
            loads()
            if k < n_units:
                quantise(k)
            for cp in range(2):
                if k == X_STEP[cp]:
                    x_quantise(cp)
            if k == X_STEP[1]:
                x_by_parity()
            if k >= 1 and k - 1 < n_units and units[k - 1][0] == "v" and units[k - 1][2] == 1:
                add_bias(units[k - 1][1])
            if 0 <= i + AHEAD_P < N_PAIR:
                project(i + AHEAD_P)
            if k < n_units and units[k][0] == "v":
                multiply(k)
            regroup_t(k + AHEAD_S + 1)
            if 0 <= i < N_PAIR:
                regroup_g(k + POOL_AHEAD)
                tables_times(i)
                turn(i)
